import numpy as np
import ml_dtypes


def mxq(x, axis, fmt="e4m3"):
    dtype, down = {"e4m3": (ml_dtypes.float8_e4m3fn, 7), "e5m2": (ml_dtypes.float8_e5m2, 14)}[fmt]
    v = np.moveaxis(np.asarray(x, np.float32).astype(ml_dtypes.bfloat16).astype(np.float64), axis, -1)
    blocks = v.reshape(v.shape[:-1] + (-1, 32))
    amax = np.abs(blocks).max(-1, keepdims=True)
    byte = np.maximum(np.where(amax > 0, np.frexp(amax)[1] - 1 + 127, 0) - down, 1)
    scale = np.exp2(byte - 127.0)
    codes = (blocks / scale).astype(np.float32).astype(dtype).astype(np.float64)
    return np.moveaxis((codes * scale).reshape(v.shape), -1, axis)


WIDE = False


def mx_kscale(k):
    if not WIDE:
        return np.ones(k)
    levels = np.array([10, -10, 5, -5, 0])
    if k % 512:
        return np.exp2(np.random.permutation(np.resize(levels, k // 32))).repeat(32)
    a = np.empty((k // 512, 16))
    for p in range(k // 512):
        a[p, :8] = np.random.permutation(np.resize(levels, 8))
        for g in range(8):
            far = levels[np.abs(levels - a[p, g]) >= 10]
            a[p, g + 8] = far[np.random.randint(len(far))]
    return np.exp2(a.ravel()).repeat(32)


BF16 = ml_dtypes.bfloat16


def bf(x):
    return np.asarray(x, np.float32).astype(BF16)


def f64(x):
    return np.asarray(x).astype(np.float64)


B, T, HID, H, NOPE, ROPE, VD, KV_LORA = 1, 512, 2048, 16, 64, 128, 128, 512
QK = NOPE + ROPE
HALF = ROPE // 2


def rope(x, cos, sin):
    c = cos[None, :, None, :]
    s = sin[None, :, None, :]
    x1, x2 = x[..., 0::2], x[..., 1::2]
    o1 = x1 * c - x2 * s
    o2 = x1 * s + x2 * c
    return np.stack([o1, o2], axis=-1).reshape(x.shape)


def draw0():
    s = mx_kscale(HID)
    ang = np.random.uniform(-np.pi, np.pi, (T, HALF))
    return {"hidden_states": bf(np.random.standard_normal((B, T, HID)) * s),
            "rope_cos": bf(np.cos(ang)), "rope_sin": bf(np.sin(ang)),
            "Wq": bf(np.random.standard_normal((HID, H * QK)) / np.sqrt(HID) / s[:, None])}


def core(hidden_states, rope_cos, rope_sin, Wq):
    q = (mxq(f64(hidden_states), 2, "e4m3") @ mxq(f64(Wq), 0, "e4m3")).reshape(B, T, H, QK)
    q_nope, q_rope = q[..., :NOPE], q[..., NOPE:]
    q_rope = rope(q_rope, f64(rope_cos), f64(rope_sin))
    return np.concatenate([q_nope, q_rope], axis=-1)


def e4m3fn_bytes(y):
    return np.clip(np.asarray(y, np.float64), -448.0, 448.0).astype(np.float32).astype(ml_dtypes.float8_e4m3fn).view(np.uint8)


def e4m3fn_values(b):
    return np.asarray(b, np.uint8).view(ml_dtypes.float8_e4m3fn).astype(np.float64)


def setup_inputs():
    d = draw0()
    x0 = np.asarray(d['Wq']).astype(np.float64)
    s = (np.max(np.abs(x0), axis=(1,), keepdims=True) / 448.0).astype(np.float32)
    out = {}
    for k, v in d.items():
        if k == 'Wq':
            out['Wq_bytes'] = e4m3fn_bytes(x0 / s.astype(np.float64))
            out['Wq_scale'] = s
        else:
            out[k] = v
    return out


def reference(hidden_states, rope_cos, rope_sin, Wq_bytes, Wq_scale):
    return core(hidden_states, rope_cos, rope_sin, e4m3fn_values(Wq_bytes) * Wq_scale.astype(np.float64))

@@ -1,0 +1,448 @@
+from contextlib import ExitStack
+
+import concourse.mybir as mybir
+from concourse.masks import make_identity
+
+F32 = mybir.dt.float32
+BF16 = mybir.dt.bfloat16
+U32 = mybir.dt.uint32
+U8 = mybir.dt.uint8
+FP8 = mybir.dt.float8_e4m3fn
+FP8X4 = mybir.dt.float8_e4m3fn_x4
+ALU = mybir.AluOpType
+ACT = mybir.ActivationFunctionType
+
+T, HID, H, NOPE, ROPE = 512, 2048, 16, 64, 128
+QK = NOPE + ROPE
+HALF = ROPE // 2
+P = 128
+PACK = 4
+K_PASS = P * PACK
+G = HID // K_PASS
+MT = T // P
+
+FLOPS = 2 * T * HID * H * QK
+
+GROUP_HEADS = (4, 4, 4, 2, 2)
+V_WIDEN = {0: (2, 3)}
+S_ROPE = ()
+ROPE_BUFS = 4
+NOPE_BUFS = 2
+MISC_BUFS = 2
+PLANE_BUFS = 4
+NE_LAG = 3
+TABLE_STEP = 1
+SPLIT_LOADS = 1
+GRPN_BUFS = 6
+X_LAG = {"S": 1, "PE": 3}
+Q_LAG = 2
+POOL_ADDS = (2, 2, 2, 2, 2)
+SPLIT_ADD = ()
+FAST = True
+HS_COPY_ON_S = ((0, 1), (1, 1), (2, 1), (3, 1))
+
+
+NOPE_PATHS = "VVVVVSVSVSVSVSVSVSVS"
+LOAD_ORDER = ("w0", "w1", "h0", "cs", "h1", "w2", "h2", "h3")
+
+
+def nope_path(c):
+    return NOPE_PATHS[c]
+
+
+def tile_multilatentattention_pb_kernel(tc, hidden_states, rope_cos, rope_sin, Wq_bytes, Wq_scale, out):
+    nc = tc.nc
+    hs_v = hidden_states.rearrange("b (m p) k -> (b m) p k", p=P)
+    w_v = Wq_bytes.rearrange("(g p t) n -> g p t n", p=P, t=PACK)
+    sc_v = Wq_scale.rearrange("(g p t) o -> p g (t o)", p=P, t=PACK)
+    cos_v = rope_cos.rearrange("(m p) i -> p m i", p=P)
+    sin_v = rope_sin.rearrange("(m p) i -> p m i", p=P)
+    out_v = out.rearrange("b (m p) h d -> (b m) p (h d)", p=P)
+
+    groups = []
+    first = 0
+    for heads in GROUP_HEADS:
+        groups.append((first, heads))
+        first += heads
+    chunks = [(j, g) for j in range(len(groups)) for g in range(G)]
+    units = [(j, m) for j in range(len(groups)) for m in range(MT)]
+    n = len(chunks)
+
+    with ExitStack() as ctx:
+        const = ctx.enter_context(tc.tile_pool(name="const", bufs=1))
+        work = ctx.enter_context(tc.tile_pool(name="work", bufs=3))
+        ps = ctx.enter_context(tc.psum_pool(name="ps", bufs=3))
+
+        ident_f = const.tile([P, P], F32, name="ident_f")
+        make_identity(nc, ident_f[:])
+        ident_b = const.tile([P, P], BF16, name="ident_b")
+        make_identity(nc, ident_b[:])
+
+        ctx.enter_context(tc.manual_schedule())
+
+        warm_i = const.tile([P, 1], F32, name="warm_i")
+        warm_o = const.tile([P, 1], F32, name="warm_o")
+        nc.vector.memset(warm_i[:], 0.0)
+        nc.scalar.activation(out=warm_o[:], in_=warm_i[:], func=ACT.Copy)
+
+        sc = const.tile([P, G, PACK], F32, name="sc")
+        cos_sb = const.tile([P, MT, HALF], BF16, name="cos_sb")
+        sin_sb = const.tile([P, MT, HALF], BF16, name="sin_sb")
+        c2 = const.tile([P, MT, ROPE], F32, name="c2")
+        s2 = const.tile([P, MT, ROPE], F32, name="s2")
+        hs_codes = const.tile([P, MT, G * P], U32, name="hs_codes", align_bytes=64)
+        hs_scales = const.tile([P, MT, G * P], U8, name="hs_scales", align_bytes=64)
+
+        wb = {}
+        pis = {}
+        hs_raw = {}
+        planes = {}
+        grp_r = {}
+        grp_n = {}
+        wc = {}
+        xts = {}
+        hs_grp = {}
+        acc_r = {}
+        acc_n = {}
+        tmp_a = {}
+        tmp_b = {}
+        o_t = {}
+
+        def load_w(c):
+            j, g = chunks[c]
+            h0, nh = groups[j]
+            cols = slice(h0 * QK, (h0 + nh) * QK)
+            if c < SPLIT_LOADS:
+                wb[c] = []
+                for t in range(PACK):
+                    one = const.tile([P, nh * QK], U8, name="wq_bytes_%d_%d" % (c, t))
+                    nc.sync.dma_start(out=one[:], in_=w_v[g][:, t, cols])
+                    wb[c].append(one[:])
+            else:
+                whole = const.tile([P, PACK, nh * QK], U8, name="wq_bytes_%d" % c)
+                nc.sync.dma_start(out=whole[:], in_=w_v[g][:, :, cols])
+                wb[c] = [whole[:, t, :] for t in range(PACK)]
+
+        def load_hs(m):
+            t = const.tile([P, HID], BF16, name="hs_raw_%d" % m)
+            nc.sync.dma_start(out=t[:], in_=hs_v[m])
+            hs_raw[m] = t
+
+        nc.sync.dma_start(out=sc[:], in_=sc_v)
+        loaded = 0
+        for item in LOAD_ORDER:
+            if item == "cs":
+                nc.sync.dma_start(out=cos_sb[:], in_=cos_v)
+                nc.sync.dma_start(out=sin_sb[:], in_=sin_v)
+            elif item.startswith("w"):
+                load_w(int(item[1:]))
+                loaded += 1
+            else:
+                load_hs(int(item[1:]))
+        for c in range(loaded, n):
+            load_w(c)
+
+        def widen(c, t):
+            j, g = chunks[c]
+            nh = groups[j][1]
+            if c not in planes:
+                planes[c] = work.tile([P, PACK, nh * QK], BF16, name="planes", tag="planes", bufs=PLANE_BUFS)
+            src = wb[c][t].bitcast(FP8)
+            dst = planes[c][:, t, :]
+            if t in V_WIDEN.get(c, ()):
+                nc.vector.tensor_scalar(out=dst, in0=src, scalar1=sc[:, g, t : t + 1], scalar2=None, op0=ALU.mult)
+            else:
+                nc.scalar.activation(out=dst, in_=src, func=ACT.Copy, scale=sc[:, g, t : t + 1])
+
+        def plane_view(c):
+            return planes[c][:].rearrange("p t (h d) -> p h d t", d=QK)
+
+        def inter_rope(c):
+            nh = groups[chunks[c][0]][1]
+            grp_r[c] = work.tile([P, nh * ROPE * PACK], BF16, name="grp_r", tag="grp_r", bufs=3, align_bytes=64)
+            if FAST:
+                dst = grp_r[c][:].rearrange("p (h c i t) -> p h c t i", h=nh, i=4, t=PACK)
+                src = planes[c][:].rearrange("p t (h d) -> p t h d", d=QK)[:, :, :, NOPE:QK].rearrange("p t h (c i) -> p h c t i", i=4)
+            else:
+                dst = grp_r[c][:].rearrange("p (h d t) -> p h d t", h=nh, t=PACK)
+                src = plane_view(c)[:, :, NOPE:QK, :]
+            if c in S_ROPE:
+                nc.scalar.copy(out=dst, in_=src)
+            else:
+                nc.vector.tensor_copy(out=dst, in_=src)
+
+        def nope_views(c):
+            nh = groups[chunks[c][0]][1]
+            if c not in grp_n:
+                grp_n[c] = work.tile([P, nh * NOPE * PACK], BF16, name="grp_n", tag="grp_n", bufs=GRPN_BUFS, align_bytes=64)
+            return grp_n[c][:].rearrange("p (h d t) -> p h d t", h=nh, t=PACK), plane_view(c)[:, :, 0:NOPE, :]
+
+        def inter_nope_pe(c):
+            nh = groups[chunks[c][0]][1]
+            src = plane_view(c)[:, :, 0:NOPE, :]
+            pis[c] = ps.tile([P, nh * NOPE * PACK], BF16, name="pi", tag="misc", bufs=MISC_BUFS)
+            for a in range(nh // 2):
+                nc.tensor.matmul(
+                    out=pis[c][:, a * 512 : (a + 1) * 512].rearrange("p (h d t) -> p h d t", h=2, t=PACK),
+                    lhsT=ident_b[:],
+                    rhs=src[:, 2 * a : 2 * a + 2, :, :],
+                    start=True,
+                    stop=True,
+                )
+
+        def inter_nope(c, path):
+            dst, src = nope_views(c)
+            if path == "V" and FAST:
+                nh = groups[chunks[c][0]][1]
+                nc.vector.tensor_copy(
+                    out=grp_n[c][:].rearrange("p (h c i t) -> p h c t i", h=nh, i=4, t=PACK),
+                    in_=planes[c][:].rearrange("p t (h d) -> p t h d", d=QK)[:, :, :, 0:NOPE].rearrange("p t h (c i) -> p h c t i", i=4),
+                )
+            elif path == "V":
+                nc.vector.tensor_copy(out=dst, in_=src)
+            elif path == "S":
+                nc.scalar.copy(out=dst, in_=src)
+            else:
+                nc.scalar.copy(out=grp_n[c][:], in_=pis[c][:])
+
+        def codes_of(j):
+            if j not in wc:
+                nh = groups[j][1]
+                wc[j] = (
+                    work.tile([P, G, nh * ROPE], U32, name="wc_r", tag="wc_r", bufs=3, align_bytes=64),
+                    work.tile([P, G, nh * ROPE], U8, name="ws_r", tag="ws_r", bufs=3, align_bytes=64),
+                    work.tile([P, G, nh * NOPE], U32, name="wc_n", tag="wc_n", bufs=3, align_bytes=64),
+                    work.tile([P, G, nh * NOPE], U8, name="ws_n", tag="ws_n", bufs=3, align_bytes=64),
+                )
+            return wc[j]
+
+        def quant_rope(c):
+            j, g = chunks[c]
+            t = codes_of(j)
+            nc.vector.quantize_mx(out=t[0][:, g, :].bitcast(FP8X4), scales=t[1][:, g, :], in_=grp_r[c][:])
+
+        def quant_nope(c):
+            j, g = chunks[c]
+            t = codes_of(j)
+            nc.vector.quantize_mx(out=t[2][:, g, :].bitcast(FP8X4), scales=t[3][:, g, :], in_=grp_n[c][:])
+
+        def hs_transposes(m):
+            words = hs_raw[m][:].bitcast(F32)
+            xts[m] = []
+            for half in range(2):
+                if half == 0:
+                    xt = ps.tile([P, 2, 2, P], F32, name="xt", tag="misc", bufs=MISC_BUFS)
+                else:
+                    xt = ps.tile([P, 2, 2, P], F32, name="xt", tag="acc_n", bufs=NOPE_BUFS)
+                for g2 in range(2):
+                    g = 2 * half + g2
+                    for u in range(2):
+                        nc.tensor.transpose(xt[:, g2, u, :], words[:, 256 * g + u : 256 * (g + 1) : 2], ident_f[:])
+                xts[m].append(xt)
+
+        def hs_copy(m, half):
+            if m not in hs_grp:
+                hs_grp[m] = work.tile([P, G * P * PACK], BF16, name="hs_grp", tag="hs_grp", bufs=2, align_bytes=64)
+            dst = hs_grp[m][:].bitcast(F32).rearrange("p (g r u) -> p g r u", g=G, u=2)
+            eng_copy = nc.scalar.copy if (m, half) in HS_COPY_ON_S else nc.vector.tensor_copy
+            eng_copy(out=dst[:, 2 * half : 2 * half + 2, :, :], in_=xts[m][half][:].rearrange("p g u r -> p g r u"))
+
+        def hs_quant(m):
+            nc.vector.quantize_mx(out=hs_codes[:, m, :].bitcast(FP8X4), scales=hs_scales[:, m, :], in_=hs_grp[m][:])
+
+        def tables():
+            cq = cos_sb[:].rearrange("p m i -> p (m i)").unsqueeze(2)
+            sq = sin_sb[:].rearrange("p m i -> p (m i)").unsqueeze(2)
+            c2v = c2[:].rearrange("p m (i e) -> p (m i) e", e=2)
+            s2v = s2[:].rearrange("p m (i e) -> p (m i) e", e=2)
+            nc.vector.tensor_copy(out=c2v, in_=cq.to_broadcast([P, MT * HALF, 2]))
+            nc.vector.tensor_scalar(out=s2v[:, :, 0:1], in0=sq, scalar1=-1.0, scalar2=None, op0=ALU.mult)
+            nc.vector.tensor_copy(out=s2v[:, :, 1:2], in_=sq)
+
+        def mm_pass(k, rope, g):
+            j, m = units[k]
+            nh = groups[j][1]
+            t = codes_of(j)
+            if rope:
+                if k not in acc_r:
+                    acc_r[k] = ps.tile([P, nh * ROPE], F32, name="acc_r", tag="acc_r", bufs=ROPE_BUFS)
+                acc, cod, sca = acc_r[k][:], t[0], t[1]
+            else:
+                if k % 2 == 0 and k not in acc_n:
+                    pair = ps.tile([P, 2, nh * NOPE], F32, name="acc_n", tag="acc_n", bufs=NOPE_BUFS)
+                    acc_n[k] = pair[:, 0, :]
+                    acc_n[k + 1] = pair[:, 1, :]
+                acc, cod, sca = acc_n[k], t[2], t[3]
+            nc.tensor.matmul_mx(
+                out=acc,
+                lhsT=hs_codes[:, m, g * P : (g + 1) * P].bitcast(FP8X4),
+                lhsT_scale=hs_scales[:, m, g * P : (g + 1) * P],
+                rhs=cod[:, g, :].bitcast(FP8X4),
+                rhs_scale=sca[:, g, :],
+                start=(g == 0),
+                stop=(g == G - 1),
+            )
+
+        def rope_a(k):
+            j, m = units[k]
+            nh = groups[j][1]
+            tmp_a[k] = work.tile([P, nh, ROPE], F32, name="tmp_a", tag="tmp_a", bufs=4)
+            nc.vector.tensor_tensor(
+                out=tmp_a[k][:],
+                in0=acc_r[k][:].rearrange("p (h d) -> p h d", h=nh),
+                in1=c2[:, m, :].unsqueeze(1).to_broadcast([P, nh, ROPE]),
+                op=ALU.mult,
+            )
+
+        def rope_b(k):
+            j, m = units[k]
+            nh = groups[j][1]
+            tmp_b[k] = work.tile([P, nh, ROPE], F32, name="tmp_b", tag="tmp_b", bufs=4)
+            nc.vector.tensor_tensor(
+                out=tmp_b[k][:].rearrange("p h (i e) -> p h i e", e=2),
+                in0=acc_r[k][:].rearrange("p (h i e) -> p h i e", h=nh, e=2)[:, :, :, ::-1],
+                in1=s2[:, m, :].rearrange("p (i e) -> p i e", e=2).unsqueeze(1).to_broadcast([P, nh, HALF, 2]),
+                op=ALU.mult,
+            )
+
+        def o_of(k):
+            if k not in o_t:
+                nh = groups[units[k][0]][1]
+                o_t[k] = work.tile([P, nh, QK], F32, name="o_t", tag="o_t", bufs=8)
+            return o_t[k]
+
+        def rope_add(k, eng, lo=0, hi=None):
+            nh = groups[units[k][0]][1]
+            top = nh if hi is None else hi
+            eng.tensor_tensor(out=o_of(k)[:, lo:top, NOPE:QK], in0=tmp_a[k][:, lo:top, :], in1=tmp_b[k][:, lo:top, :], op=ALU.add)
+
+        def nope_out(k):
+            nh = groups[units[k][0]][1]
+            nc.scalar.copy(out=o_of(k)[:, :, 0:NOPE], in_=acc_n[k].rearrange("p (h d) -> p h d", h=nh))
+
+        def store(k):
+            j, m = units[k]
+            h0, nh = groups[j]
+            nc.sync.dma_start(out=out_v[m][:, h0 * QK : (h0 + nh) * QK], in_=o_t[k][:].rearrange("p h d -> p (h d)"))
+
+        st = {"mm_r": 0, "mm_n": 0, "epi": 0, "add": 0, "ne": 0, "store": 0, "hs_ready": 0}
+        qr_done = [0] * len(groups)
+        qn_done = [0] * len(groups)
+        pass_r = [0] * len(units)
+        pass_n = [0] * len(units)
+
+        def emit_some(rope):
+            done, passes = (qr_done, pass_r) if rope else (qn_done, pass_n)
+            lo, hi = (st["epi"], st["epi"] + ROPE_BUFS) if rope else (st["mm_n"], st["ne"] - st["ne"] % 2 + 2 * NOPE_BUFS)
+            for k in range(lo, min(hi, len(units))):
+                j, m = units[k]
+                if m >= st["hs_ready"] or (not rope and st["hs_ready"] < MT):
+                    break
+                if passes[k] == 0 and done[j] == 0:
+                    break
+                if not rope and done[j] < G:
+                    break
+                while passes[k] < done[j]:
+                    mm_pass(k, rope, passes[k])
+                    passes[k] += 1
+            key = "mm_r" if rope else "mm_n"
+            while st[key] < len(units) and passes[st[key]] == G:
+                st[key] += 1
+
+        def emit_mm():
+            emit_some(False)
+            emit_some(True)
+
+        ne_step = {}
+        half_done = {}
+        batch_ready = []
+        x_done = {}
+        q_next = [0]
+
+        def do_quant_nope(limit_step):
+            while q_next[0] < n and q_next[0] in x_done and (q_next[0] + Q_LAG <= limit_step or limit_step >= n):
+                quant_nope(q_next[0])
+                qn_done[chunks[q_next[0]][0]] += 1
+                q_next[0] += 1
+
+        s = 0
+        while st["store"] < len(units):
+            prev = s - 1 if 0 <= s - 1 < n else None
+            if s < n:
+                widen(s, 0)
+                widen(s, 1)
+            if prev is not None and nope_path(prev) == "PE":
+                inter_nope_pe(prev)
+            for c in range(min(s, n)):
+                path = nope_path(c)
+                if c not in x_done and path != "V" and (c + X_LAG[path] <= s or s >= n):
+                    inter_nope(c, path)
+                    x_done[c] = s
+            if prev is not None and prev in S_ROPE:
+                inter_rope(prev)
+            if s < n:
+                widen(s, 2)
+                widen(s, 3)
+            do_hs = 1 <= s <= MT
+            if prev is not None and prev not in S_ROPE:
+                inter_rope(prev)
+            if s == TABLE_STEP:
+                tables()
+            if prev is None:
+                do_quant_nope(s)
+                emit_mm()
+            if batch_ready:
+                j = batch_ready.pop(0)
+                for m in range(MT):
+                    k = j * MT + m
+                    rope_a(k)
+                    rope_b(k)
+                    st["epi"] += 1
+                    if m < POOL_ADDS[j]:
+                        rope_add(k, nc.gpsimd)
+                        st["add"] += 1
+                    elif m == POOL_ADDS[j] and j in SPLIT_ADD:
+                        rope_add(k, nc.gpsimd, 0, groups[j][1] // 2)
+                        half_done[k] = True
+            if do_hs:
+                hs_copy(s - 1, 0)
+            if prev is not None and nope_path(prev) == "V":
+                inter_nope(prev, "V")
+                x_done[prev] = s
+            do_quant_nope(s)
+            if do_hs:
+                hs_copy(s - 1, 1)
+            while st["add"] < st["epi"]:
+                if st["add"] in half_done:
+                    rope_add(st["add"], nc.vector, groups[units[st["add"]][0]][1] // 2, None)
+                else:
+                    rope_add(st["add"], nc.vector)
+                st["add"] += 1
+            if prev is not None:
+                quant_rope(prev)
+                qr_done[chunks[prev][0]] += 1
+                if chunks[prev][1] == G - 1:
+                    batch_ready.append(chunks[prev][0])
+            if do_hs:
+                hs_quant(s - 1)
+                st["hs_ready"] = s
+            emit_mm()
+            if s == 0:
+                hs_transposes(0)
+            if s + 1 < MT:
+                hs_transposes(s + 1)
+            progress = True
+            while progress:
+                progress = False
+                for k in range(st["ne"], st["mm_n"]):
+                    if k not in ne_step:
+                        ne_step[k] = s
+                if st["ne"] < st["mm_n"] and (s >= ne_step[st["ne"]] + NE_LAG or s >= n):
+                    nope_out(st["ne"])
+                    st["ne"] += 1
+                    emit_some(False)
+                    progress = True
+            while st["store"] < st["add"] and st["store"] < st["ne"]:
+                store(st["store"])
+                st["store"] += 1
+            s += 1

@@ -24,30 +24,18 @@ MT = T // P
 FLOPS = 2 * T * HID * H * QK
 
 GROUP_HEADS = (4, 4, 4, 2, 2)
-V_WIDEN = {0: (2, 3)}
-S_ROPE = ()
-ROPE_BUFS = 4
-NOPE_BUFS = 2
-MISC_BUFS = 2
-PLANE_BUFS = 4
-NE_LAG = 3
-TABLE_STEP = 1
-SPLIT_LOADS = 1
-GRPN_BUFS = 6
-X_LAG = {"S": 1, "PE": 3}
-Q_LAG = 2
-POOL_ADDS = (2, 2, 2, 2, 2)
-SPLIT_ADD = ()
-FAST = True
-HS_COPY_ON_S = ((0, 1), (1, 1), (2, 1), (3, 1))
-
-
-NOPE_PATHS = "VVVVVSVSVSVSVSVSVSVS"
-LOAD_ORDER = ("w0", "w1", "h0", "cs", "h1", "w2", "h2", "h3")
-
-
-def nope_path(c):
-    return NOPE_PATHS[c]
+RUN = 2
+V_PLANES = (2, 2, 2, 2, 1, 0, 1, 0, 1, 0, 1, 0, 0, 0, 0, 0, 0, 0, 0, 0)
+PE_FROM = 4
+ROPE_PE_FROM = 20
+G_ROWS = 12
+EVAC_LAG = 1
+ROPE_LAG = 6
+HS_ON_S = (0, 1)
+LOAD_ORDER = ("w0", "w1", "h0", "cs", "w2", "h1", "w3", "h2", "w4", "h3")
+TABLE_STEP = 3
+NOUT_LAG = 1
+HS_STEP = 1
 
 
 def tile_multilatentattention_pb_kernel(tc, hidden_states, rope_cos, rope_sin, Wq_bytes, Wq_scale, out):
@@ -64,14 +52,12 @@ def tile_multilatentattention_pb_kernel(tc, hidden_states, rope_cos, rope_sin, W
     for heads in GROUP_HEADS:
         groups.append((first, heads))
         first += heads
-    chunks = [(j, g) for j in range(len(groups)) for g in range(G)]
-    units = [(j, m) for j in range(len(groups)) for m in range(MT)]
-    n = len(chunks)
+    n = len(groups) * G
 
     with ExitStack() as ctx:
         const = ctx.enter_context(tc.tile_pool(name="const", bufs=1))
         work = ctx.enter_context(tc.tile_pool(name="work", bufs=3))
-        ps = ctx.enter_context(tc.psum_pool(name="ps", bufs=3))
+        ps = ctx.enter_context(tc.psum_pool(name="ps", bufs=2))
 
         ident_f = const.tile([P, P], F32, name="ident_f")
         make_identity(nc, ident_f[:])
@@ -82,6 +68,7 @@ def tile_multilatentattention_pb_kernel(tc, hidden_states, rope_cos, rope_sin, W
 
         warm_i = const.tile([P, 1], F32, name="warm_i")
         warm_o = const.tile([P, 1], F32, name="warm_o")
+        gate = const.tile([P, 1], F32, name="gate")
         nc.vector.memset(warm_i[:], 0.0)
         nc.scalar.activation(out=warm_o[:], in_=warm_i[:], func=ACT.Copy)
 
@@ -94,25 +81,29 @@ def tile_multilatentattention_pb_kernel(tc, hidden_states, rope_cos, rope_sin, W
         hs_scales = const.tile([P, MT, G * P], U8, name="hs_scales", align_bytes=64)
 
         wb = {}
-        pis = {}
         hs_raw = {}
         planes = {}
         grp_r = {}
         grp_n = {}
+        pis = {}
+        pir = {}
         wc = {}
         xts = {}
         hs_grp = {}
         acc_r = {}
         acc_n = {}
-        tmp_a = {}
-        tmp_b = {}
-        o_t = {}
+        ta = {}
+        tb = {}
+        ot = {}
+
+        def heads_of(c):
+            return groups[c // G][1]
 
         def load_w(c):
-            j, g = chunks[c]
+            j, g = c // G, c % G
             h0, nh = groups[j]
             cols = slice(h0 * QK, (h0 + nh) * QK)
-            if c < SPLIT_LOADS:
+            if c == 0:
                 wb[c] = []
                 for t in range(PACK):
                     one = const.tile([P, nh * QK], U8, name="wq_bytes_%d_%d" % (c, t))
@@ -124,9 +115,8 @@ def tile_multilatentattention_pb_kernel(tc, hidden_states, rope_cos, rope_sin, W
                 wb[c] = [whole[:, t, :] for t in range(PACK)]
 
         def load_hs(m):
-            t = const.tile([P, HID], BF16, name="hs_raw_%d" % m)
-            nc.sync.dma_start(out=t[:], in_=hs_v[m])
-            hs_raw[m] = t
+            hs_raw[m] = const.tile([P, HID], BF16, name="hs_raw_%d" % m)
+            nc.sync.dma_start(out=hs_raw[m][:], in_=hs_v[m])
 
         nc.sync.dma_start(out=sc[:], in_=sc_v)
         loaded = 0
@@ -142,45 +132,30 @@ def tile_multilatentattention_pb_kernel(tc, hidden_states, rope_cos, rope_sin, W
         for c in range(loaded, n):
             load_w(c)
 
-        def widen(c, t):
-            j, g = chunks[c]
-            nh = groups[j][1]
+        def widen(c, t, on_vector):
+            g = c % G
+            nh = heads_of(c)
             if c not in planes:
-                planes[c] = work.tile([P, PACK, nh * QK], BF16, name="planes", tag="planes", bufs=PLANE_BUFS)
+                planes[c] = work.tile([P, PACK, nh * QK], BF16, name="planes", tag="planes", bufs=4)
             src = wb[c][t].bitcast(FP8)
             dst = planes[c][:, t, :]
-            if t in V_WIDEN.get(c, ()):
+            if on_vector:
                 nc.vector.tensor_scalar(out=dst, in0=src, scalar1=sc[:, g, t : t + 1], scalar2=None, op0=ALU.mult)
             else:
                 nc.scalar.activation(out=dst, in_=src, func=ACT.Copy, scale=sc[:, g, t : t + 1])
 
-        def plane_view(c):
-            return planes[c][:].rearrange("p t (h d) -> p h d t", d=QK)
+        def inter_v(c, lo, hi, store, tag, bufs):
+            nh = heads_of(c)
+            store[c] = work.tile([P, nh * (hi - lo) * PACK], BF16, name=tag, tag=tag, bufs=bufs, align_bytes=64)
+            nc.vector.tensor_copy(
+                out=store[c][:].rearrange("p (h c i t) -> p h c t i", h=nh, i=4, t=PACK),
+                in_=planes[c][:].rearrange("p t (h d) -> p t h d", d=QK)[:, :, :, lo:hi].rearrange("p t h (c i) -> p h c t i", i=4),
+            )
 
-        def inter_rope(c):
-            nh = groups[chunks[c][0]][1]
-            grp_r[c] = work.tile([P, nh * ROPE * PACK], BF16, name="grp_r", tag="grp_r", bufs=3, align_bytes=64)
-            if FAST:
-                dst = grp_r[c][:].rearrange("p (h c i t) -> p h c t i", h=nh, i=4, t=PACK)
-                src = planes[c][:].rearrange("p t (h d) -> p t h d", d=QK)[:, :, :, NOPE:QK].rearrange("p t h (c i) -> p h c t i", i=4)
-            else:
-                dst = grp_r[c][:].rearrange("p (h d t) -> p h d t", h=nh, t=PACK)
-                src = plane_view(c)[:, :, NOPE:QK, :]
-            if c in S_ROPE:
-                nc.scalar.copy(out=dst, in_=src)
-            else:
-                nc.vector.tensor_copy(out=dst, in_=src)
-
-        def nope_views(c):
-            nh = groups[chunks[c][0]][1]
-            if c not in grp_n:
-                grp_n[c] = work.tile([P, nh * NOPE * PACK], BF16, name="grp_n", tag="grp_n", bufs=GRPN_BUFS, align_bytes=64)
-            return grp_n[c][:].rearrange("p (h d t) -> p h d t", h=nh, t=PACK), plane_view(c)[:, :, 0:NOPE, :]
-
-        def inter_nope_pe(c):
-            nh = groups[chunks[c][0]][1]
-            src = plane_view(c)[:, :, 0:NOPE, :]
-            pis[c] = ps.tile([P, nh * NOPE * PACK], BF16, name="pi", tag="misc", bufs=MISC_BUFS)
+        def ident_nope(c):
+            nh = heads_of(c)
+            src = planes[c][:].rearrange("p t (h d) -> p h d t", d=QK)[:, :, 0:NOPE, :]
+            pis[c] = ps.tile([P, nh * NOPE * PACK], BF16, name="pi", tag="misc", bufs=2)
             for a in range(nh // 2):
                 nc.tensor.matmul(
                     out=pis[c][:, a * 512 : (a + 1) * 512].rearrange("p (h d t) -> p h d t", h=2, t=PACK),
@@ -190,20 +165,28 @@ def tile_multilatentattention_pb_kernel(tc, hidden_states, rope_cos, rope_sin, W
                     stop=True,
                 )
 
-        def inter_nope(c, path):
-            dst, src = nope_views(c)
-            if path == "V" and FAST:
-                nh = groups[chunks[c][0]][1]
-                nc.vector.tensor_copy(
-                    out=grp_n[c][:].rearrange("p (h c i t) -> p h c t i", h=nh, i=4, t=PACK),
-                    in_=planes[c][:].rearrange("p t (h d) -> p t h d", d=QK)[:, :, :, 0:NOPE].rearrange("p t h (c i) -> p h c t i", i=4),
+        def evac_nope(c):
+            nh = heads_of(c)
+            grp_n[c] = work.tile([P, nh * NOPE * PACK], BF16, name="grp_n", tag="grp_n", bufs=4, align_bytes=64)
+            nc.scalar.copy(out=grp_n[c][:], in_=pis[c][:])
+
+        def ident_rope(c):
+            nh = heads_of(c)
+            src = planes[c][:].rearrange("p t (h d) -> p h d t", d=QK)[:, :, NOPE:QK, :]
+            pir[c] = ps.tile([P, nh * ROPE * PACK], BF16, name="pir", tag="misc", bufs=2)
+            for a in range(nh):
+                nc.tensor.matmul(
+                    out=pir[c][:, a * 512 : (a + 1) * 512].rearrange("p (d t) -> p d t", t=PACK),
+                    lhsT=ident_b[:],
+                    rhs=src[:, a, :, :],
+                    start=True,
+                    stop=True,
                 )
-            elif path == "V":
-                nc.vector.tensor_copy(out=dst, in_=src)
-            elif path == "S":
-                nc.scalar.copy(out=dst, in_=src)
-            else:
-                nc.scalar.copy(out=grp_n[c][:], in_=pis[c][:])
+
+        def evac_rope(c):
+            nh = heads_of(c)
+            grp_r[c] = work.tile([P, nh * ROPE * PACK], BF16, name="grp_r", tag="grp_r", bufs=3, align_bytes=64)
+            nc.scalar.copy(out=grp_r[c][:], in_=pir[c][:])
 
         def codes_of(j):
             if j not in wc:
@@ -216,24 +199,19 @@ def tile_multilatentattention_pb_kernel(tc, hidden_states, rope_cos, rope_sin, W
                 )
             return wc[j]
 
-        def quant_rope(c):
-            j, g = chunks[c]
+        def quant(c, rope):
+            j, g = c // G, c % G
             t = codes_of(j)
-            nc.vector.quantize_mx(out=t[0][:, g, :].bitcast(FP8X4), scales=t[1][:, g, :], in_=grp_r[c][:])
-
-        def quant_nope(c):
-            j, g = chunks[c]
-            t = codes_of(j)
-            nc.vector.quantize_mx(out=t[2][:, g, :].bitcast(FP8X4), scales=t[3][:, g, :], in_=grp_n[c][:])
+            if rope:
+                nc.vector.quantize_mx(out=t[0][:, g, :].bitcast(FP8X4), scales=t[1][:, g, :], in_=grp_r[c][:])
+            else:
+                nc.vector.quantize_mx(out=t[2][:, g, :].bitcast(FP8X4), scales=t[3][:, g, :], in_=grp_n[c][:])
 
         def hs_transposes(m):
             words = hs_raw[m][:].bitcast(F32)
             xts[m] = []
             for half in range(2):
-                if half == 0:
-                    xt = ps.tile([P, 2, 2, P], F32, name="xt", tag="misc", bufs=MISC_BUFS)
-                else:
-                    xt = ps.tile([P, 2, 2, P], F32, name="xt", tag="acc_n", bufs=NOPE_BUFS)
+                xt = ps.tile([P, 2, 2, P], F32, name="xt", tag=("misc", "acc_n")[half], bufs=2)
                 for g2 in range(2):
                     g = 2 * half + g2
                     for u in range(2):
@@ -244,7 +222,7 @@ def tile_multilatentattention_pb_kernel(tc, hidden_states, rope_cos, rope_sin, W
             if m not in hs_grp:
                 hs_grp[m] = work.tile([P, G * P * PACK], BF16, name="hs_grp", tag="hs_grp", bufs=2, align_bytes=64)
             dst = hs_grp[m][:].bitcast(F32).rearrange("p (g r u) -> p g r u", g=G, u=2)
-            eng_copy = nc.scalar.copy if (m, half) in HS_COPY_ON_S else nc.vector.tensor_copy
+            eng_copy = nc.scalar.copy if half in HS_ON_S else nc.vector.tensor_copy
             eng_copy(out=dst[:, 2 * half : 2 * half + 2, :, :], in_=xts[m][half][:].rearrange("p g u r -> p g r u"))
 
         def hs_quant(m):
@@ -260,16 +238,16 @@ def tile_multilatentattention_pb_kernel(tc, hidden_states, rope_cos, rope_sin, W
             nc.vector.tensor_copy(out=s2v[:, :, 1:2], in_=sq)
 
         def mm_pass(k, rope, g):
-            j, m = units[k]
+            j, m = k // MT, k % MT
             nh = groups[j][1]
             t = codes_of(j)
             if rope:
                 if k not in acc_r:
-                    acc_r[k] = ps.tile([P, nh * ROPE], F32, name="acc_r", tag="acc_r", bufs=ROPE_BUFS)
+                    acc_r[k] = ps.tile([P, nh * ROPE], F32, name="acc_r", tag="acc_r", bufs=4)
                 acc, cod, sca = acc_r[k][:], t[0], t[1]
             else:
                 if k % 2 == 0 and k not in acc_n:
-                    pair = ps.tile([P, 2, nh * NOPE], F32, name="acc_n", tag="acc_n", bufs=NOPE_BUFS)
+                    pair = ps.tile([P, 2, nh * NOPE], F32, name="acc_n", tag="acc_n", bufs=2)
                     acc_n[k] = pair[:, 0, :]
                     acc_n[k + 1] = pair[:, 1, :]
                 acc, cod, sca = acc_n[k], t[2], t[3]
@@ -283,166 +261,124 @@ def tile_multilatentattention_pb_kernel(tc, hidden_states, rope_cos, rope_sin, W
                 stop=(g == G - 1),
             )
 
-        def rope_a(k):
-            j, m = units[k]
-            nh = groups[j][1]
-            tmp_a[k] = work.tile([P, nh, ROPE], F32, name="tmp_a", tag="tmp_a", bufs=4)
+        def run_tiles(r):
+            nh = groups[r * RUN // MT][1]
+            if r not in ta:
+                ta[r] = work.tile([P, RUN, nh, ROPE], F32, name="ta", tag="ta", bufs=2)
+                tb[r] = work.tile([P, RUN, nh, ROPE], F32, name="tb", tag="tb", bufs=2)
+            return nh
+
+        def out_tile(r):
+            nh = groups[r * RUN // MT][1]
+            if r not in ot:
+                ot[r] = work.tile([P, RUN, nh, QK], F32, name="ot", tag="ot", bufs=5)
+            return ot[r]
+
+        def rope_mults(k):
+            r, u, m = k // RUN, k % RUN, k % MT
+            nh = run_tiles(r)
             nc.vector.tensor_tensor(
-                out=tmp_a[k][:],
+                out=ta[r][:, u, :, :],
                 in0=acc_r[k][:].rearrange("p (h d) -> p h d", h=nh),
                 in1=c2[:, m, :].unsqueeze(1).to_broadcast([P, nh, ROPE]),
                 op=ALU.mult,
             )
-
-        def rope_b(k):
-            j, m = units[k]
-            nh = groups[j][1]
-            tmp_b[k] = work.tile([P, nh, ROPE], F32, name="tmp_b", tag="tmp_b", bufs=4)
             nc.vector.tensor_tensor(
-                out=tmp_b[k][:].rearrange("p h (i e) -> p h i e", e=2),
+                out=tb[r][:, u, :, :].rearrange("p h (i e) -> p h i e", e=2),
                 in0=acc_r[k][:].rearrange("p (h i e) -> p h i e", h=nh, e=2)[:, :, :, ::-1],
                 in1=s2[:, m, :].rearrange("p (i e) -> p i e", e=2).unsqueeze(1).to_broadcast([P, nh, HALF, 2]),
                 op=ALU.mult,
             )
 
-        def o_of(k):
-            if k not in o_t:
-                nh = groups[units[k][0]][1]
-                o_t[k] = work.tile([P, nh, QK], F32, name="o_t", tag="o_t", bufs=8)
-            return o_t[k]
-
-        def rope_add(k, eng, lo=0, hi=None):
-            nh = groups[units[k][0]][1]
-            top = nh if hi is None else hi
-            eng.tensor_tensor(out=o_of(k)[:, lo:top, NOPE:QK], in0=tmp_a[k][:, lo:top, :], in1=tmp_b[k][:, lo:top, :], op=ALU.add)
+        def rope_add(r, eng, lo, hi):
+            if hi > lo:
+                eng.tensor_tensor(
+                    out=out_tile(r)[:].rearrange("p u h d -> p (u h) d")[:, lo:hi, NOPE:QK],
+                    in0=ta[r][:].rearrange("p u h d -> p (u h) d")[:, lo:hi, :],
+                    in1=tb[r][:].rearrange("p u h d -> p (u h) d")[:, lo:hi, :],
+                    op=ALU.add,
+                )
 
         def nope_out(k):
-            nh = groups[units[k][0]][1]
-            nc.scalar.copy(out=o_of(k)[:, :, 0:NOPE], in_=acc_n[k].rearrange("p (h d) -> p h d", h=nh))
+            r, u = k // RUN, k % RUN
+            nh = groups[k // MT][1]
+            nc.scalar.copy(out=out_tile(r)[:, u, :, 0:NOPE], in_=acc_n[k].rearrange("p (h d) -> p h d", h=nh))
 
         def store(k):
-            j, m = units[k]
+            j, m = k // MT, k % MT
             h0, nh = groups[j]
-            nc.sync.dma_start(out=out_v[m][:, h0 * QK : (h0 + nh) * QK], in_=o_t[k][:].rearrange("p h d -> p (h d)"))
+            nc.sync.dma_start(out=out_v[m][:, h0 * QK : (h0 + nh) * QK], in_=ot[k // RUN][:, k % RUN, :, :].rearrange("p h d -> p (h d)"))
 
-        st = {"mm_r": 0, "mm_n": 0, "epi": 0, "add": 0, "ne": 0, "store": 0, "hs_ready": 0}
-        qr_done = [0] * len(groups)
-        qn_done = [0] * len(groups)
-        pass_r = [0] * len(units)
-        pass_n = [0] * len(units)
-
-        def emit_some(rope):
-            done, passes = (qr_done, pass_r) if rope else (qn_done, pass_n)
-            lo, hi = (st["epi"], st["epi"] + ROPE_BUFS) if rope else (st["mm_n"], st["ne"] - st["ne"] % 2 + 2 * NOPE_BUFS)
-            for k in range(lo, min(hi, len(units))):
-                j, m = units[k]
-                if m >= st["hs_ready"] or (not rope and st["hs_ready"] < MT):
-                    break
-                if passes[k] == 0 and done[j] == 0:
-                    break
-                if not rope and done[j] < G:
-                    break
-                while passes[k] < done[j]:
-                    mm_pass(k, rope, passes[k])
-                    passes[k] += 1
-            key = "mm_r" if rope else "mm_n"
-            while st[key] < len(units) and passes[st[key]] == G:
-                st[key] += 1
-
-        def emit_mm():
-            emit_some(False)
-            emit_some(True)
-
-        ne_step = {}
-        half_done = {}
-        batch_ready = []
-        x_done = {}
-        q_next = [0]
-
-        def do_quant_nope(limit_step):
-            while q_next[0] < n and q_next[0] in x_done and (q_next[0] + Q_LAG <= limit_step or limit_step >= n):
-                quant_nope(q_next[0])
-                qn_done[chunks[q_next[0]][0]] += 1
-                q_next[0] += 1
-
-        s = 0
-        while st["store"] < len(units):
-            prev = s - 1 if 0 <= s - 1 < n else None
+        n_runs = n // RUN
+        last_step = n + ROPE_LAG + 2 * RUN + 2
+        for s in range(last_step):
             if s < n:
-                widen(s, 0)
-                widen(s, 1)
-            if prev is not None and nope_path(prev) == "PE":
-                inter_nope_pe(prev)
-            for c in range(min(s, n)):
-                path = nope_path(c)
-                if c not in x_done and path != "V" and (c + X_LAG[path] <= s or s >= n):
-                    inter_nope(c, path)
-                    x_done[c] = s
-            if prev is not None and prev in S_ROPE:
-                inter_rope(prev)
-            if s < n:
-                widen(s, 2)
-                widen(s, 3)
-            do_hs = 1 <= s <= MT
-            if prev is not None and prev not in S_ROPE:
-                inter_rope(prev)
+                for t in range(PACK):
+                    widen(s, t, t >= PACK - V_PLANES[s])
+            c = s - 1
+            if ROPE_PE_FROM <= c < n:
+                ident_rope(c)
+            if PE_FROM <= c < n:
+                ident_nope(c)
+            c = s - EVAC_LAG
+            if ROPE_PE_FROM <= c < n:
+                evac_rope(c)
+            if PE_FROM <= c < n:
+                evac_nope(c)
+            m = s - 1 - HS_STEP
+            if 0 <= m < MT:
+                hs_copy(m, 0)
+                hs_copy(m, 1)
+            c = s - 1
+            if 0 <= c < n:
+                if c < ROPE_PE_FROM:
+                    inter_v(c, NOPE, QK, grp_r, "grp_r", 3)
+                if c < PE_FROM:
+                    inter_v(c, 0, NOPE, grp_n, "grp_n", 4)
             if s == TABLE_STEP:
                 tables()
-            if prev is None:
-                do_quant_nope(s)
-                emit_mm()
-            if batch_ready:
-                j = batch_ready.pop(0)
-                for m in range(MT):
-                    k = j * MT + m
-                    rope_a(k)
-                    rope_b(k)
-                    st["epi"] += 1
-                    if m < POOL_ADDS[j]:
-                        rope_add(k, nc.gpsimd)
-                        st["add"] += 1
-                    elif m == POOL_ADDS[j] and j in SPLIT_ADD:
-                        rope_add(k, nc.gpsimd, 0, groups[j][1] // 2)
-                        half_done[k] = True
-            if do_hs:
-                hs_copy(s - 1, 0)
-            if prev is not None and nope_path(prev) == "V":
-                inter_nope(prev, "V")
-                x_done[prev] = s
-            do_quant_nope(s)
-            if do_hs:
-                hs_copy(s - 1, 1)
-            while st["add"] < st["epi"]:
-                if st["add"] in half_done:
-                    rope_add(st["add"], nc.vector, groups[units[st["add"]][0]][1] // 2, None)
-                else:
-                    rope_add(st["add"], nc.vector)
-                st["add"] += 1
-            if prev is not None:
-                quant_rope(prev)
-                qr_done[chunks[prev][0]] += 1
-                if chunks[prev][1] == G - 1:
-                    batch_ready.append(chunks[prev][0])
-            if do_hs:
-                hs_quant(s - 1)
-                st["hs_ready"] = s
-            emit_mm()
-            if s == 0:
-                hs_transposes(0)
-            if s + 1 < MT:
-                hs_transposes(s + 1)
-            progress = True
-            while progress:
-                progress = False
-                for k in range(st["ne"], st["mm_n"]):
-                    if k not in ne_step:
-                        ne_step[k] = s
-                if st["ne"] < st["mm_n"] and (s >= ne_step[st["ne"]] + NE_LAG or s >= n):
-                    nope_out(st["ne"])
-                    st["ne"] += 1
-                    emit_some(False)
-                    progress = True
-            while st["store"] < st["add"] and st["store"] < st["ne"]:
-                store(st["store"])
-                st["store"] += 1
-            s += 1
+            c = s - 1 - EVAC_LAG
+            if 0 <= c < n:
+                quant(c, False)
+            k0 = s - ROPE_LAG
+            if k0 >= 0 and k0 % RUN == 0 and k0 < n:
+                r = k0 // RUN
+                rows = RUN * groups[k0 // MT][1]
+                if r > 0:
+                    prows = RUN * groups[(k0 - RUN) // MT][1]
+                    grows = prows * G_ROWS // 16
+                    rope_add(r - 1, nc.vector, grows, prows)
+                    nc.gpsimd.tensor_copy(out=gate[:], in_=ot[r - 1][:, RUN - 1, groups[(k0 - RUN) // MT][1] - 1, QK - 1 : QK])
+                    rope_add(r - 1, nc.gpsimd, 0, grows)
+                for u in range(RUN):
+                    rope_mults(k0 + u)
+                if r == n_runs - 1:
+                    rope_add(r, nc.vector, 0, rows)
+            c = s - 1
+            if 0 <= c < n:
+                quant(c, True)
+            m = s - 1 - HS_STEP
+            if 0 <= m < MT:
+                hs_quant(m)
+            m = s - HS_STEP
+            if 0 <= m < MT:
+                hs_transposes(m)
+            for k in range(n):
+                for g in range(G):
+                    if max((k // MT) * G + g + 2, k + 3, (k + 2 + HS_STEP) if k < MT else 0) == s:
+                        mm_pass(k, True, g)
+            for k in range(n):
+                j, m = k // MT, k % MT
+                if j * G + 6 + m // 2 == s:
+                    for g in range(G):
+                        mm_pass(k, False, g)
+            for k in range(n):
+                j, m = k // MT, k % MT
+                if j * G + 6 + m // 2 + NOUT_LAG == s:
+                    nope_out(k)
+            for k in range(n):
+                r = k // RUN
+                j, m = k // MT, k % MT
+                add_step = (r + 1) * RUN + ROPE_LAG if r < n_runs - 1 else r * RUN + ROPE_LAG
+                if max(add_step, j * G + 6 + m // 2 + NOUT_LAG) == s:
+                    store(k)

@@ -25,17 +25,25 @@ FLOPS = 2 * T * HID * H * QK
 
 GROUP_HEADS = (4, 4, 4, 2, 2)
 RUN = 2
-V_PLANES = (2, 2, 2, 2, 1, 0, 1, 0, 1, 0, 1, 0, 0, 0, 0, 0, 0, 0, 0, 0)
+V_PLANES = (2, 2, 2, 2, 1, 0, 1, 0, 1, 0, 0, 0, 0, 0, 0, 0, 0, 0, 0, 0)
 PE_FROM = 4
 ROPE_PE_FROM = 20
-G_ROWS = 12
-EVAC_LAG = 1
+G_ROWS = 10
+EVAC_LAG = 2
 ROPE_LAG = 6
 HS_ON_S = (0, 1)
 LOAD_ORDER = ("w0", "w1", "h0", "cs", "w2", "h1", "w3", "h2", "w4", "h3")
 TABLE_STEP = 3
 NOUT_LAG = 1
 HS_STEP = 1
+PASS_LAG = 2
+VW_AHEAD = 0
+PLANE_BUFS = 4
+OT_BUFS = 5
+GRPR_BUFS = 3
+QR_LAG = 1
+NOUT_ON_V = False
+G_ROWS_SMALL = 8
 
 
 def tile_multilatentattention_pb_kernel(tc, hidden_states, rope_cos, rope_sin, Wq_bytes, Wq_scale, out):
@@ -136,7 +144,7 @@ def tile_multilatentattention_pb_kernel(tc, hidden_states, rope_cos, rope_sin, W
             g = c % G
             nh = heads_of(c)
             if c not in planes:
-                planes[c] = work.tile([P, PACK, nh * QK], BF16, name="planes", tag="planes", bufs=4)
+                planes[c] = work.tile([P, PACK, nh * QK], BF16, name="planes", tag="planes", bufs=PLANE_BUFS)
             src = wb[c][t].bitcast(FP8)
             dst = planes[c][:, t, :]
             if on_vector:
@@ -144,12 +152,12 @@ def tile_multilatentattention_pb_kernel(tc, hidden_states, rope_cos, rope_sin, W
             else:
                 nc.scalar.activation(out=dst, in_=src, func=ACT.Copy, scale=sc[:, g, t : t + 1])
 
-        def inter_v(c, lo, hi, store, tag, bufs):
+        def inter_v(c, lo, hi, store, tag, bufs, skip=0):
             nh = heads_of(c)
             store[c] = work.tile([P, nh * (hi - lo) * PACK], BF16, name=tag, tag=tag, bufs=bufs, align_bytes=64)
             nc.vector.tensor_copy(
-                out=store[c][:].rearrange("p (h c i t) -> p h c t i", h=nh, i=4, t=PACK),
-                in_=planes[c][:].rearrange("p t (h d) -> p t h d", d=QK)[:, :, :, lo:hi].rearrange("p t h (c i) -> p h c t i", i=4),
+                out=store[c][:].rearrange("p (h c i t) -> p h c t i", h=nh, i=4, t=PACK)[:, 0 : nh - skip],
+                in_=planes[c][:].rearrange("p t (h d) -> p t h d", d=QK)[:, :, 0 : nh - skip, lo:hi].rearrange("p t h (c i) -> p h c t i", i=4),
             )
 
         def ident_nope(c):
@@ -173,20 +181,18 @@ def tile_multilatentattention_pb_kernel(tc, hidden_states, rope_cos, rope_sin, W
         def ident_rope(c):
             nh = heads_of(c)
             src = planes[c][:].rearrange("p t (h d) -> p h d t", d=QK)[:, :, NOPE:QK, :]
-            pir[c] = ps.tile([P, nh * ROPE * PACK], BF16, name="pir", tag="misc", bufs=2)
-            for a in range(nh):
-                nc.tensor.matmul(
-                    out=pir[c][:, a * 512 : (a + 1) * 512].rearrange("p (d t) -> p d t", t=PACK),
-                    lhsT=ident_b[:],
-                    rhs=src[:, a, :, :],
-                    start=True,
-                    stop=True,
-                )
+            pir[c] = ps.tile([P, ROPE * PACK], BF16, name="pir", tag="misc", bufs=2)
+            nc.tensor.matmul(
+                out=pir[c][:].rearrange("p (d t) -> p d t", t=PACK),
+                lhsT=ident_b[:],
+                rhs=src[:, nh - 1, :, :],
+                start=True,
+                stop=True,
+            )
 
         def evac_rope(c):
             nh = heads_of(c)
-            grp_r[c] = work.tile([P, nh * ROPE * PACK], BF16, name="grp_r", tag="grp_r", bufs=3, align_bytes=64)
-            nc.scalar.copy(out=grp_r[c][:], in_=pir[c][:])
+            nc.scalar.copy(out=grp_r[c][:, (nh - 1) * ROPE * PACK :], in_=pir[c][:])
 
         def codes_of(j):
             if j not in wc:
@@ -271,7 +277,7 @@ def tile_multilatentattention_pb_kernel(tc, hidden_states, rope_cos, rope_sin, W
         def out_tile(r):
             nh = groups[r * RUN // MT][1]
             if r not in ot:
-                ot[r] = work.tile([P, RUN, nh, QK], F32, name="ot", tag="ot", bufs=5)
+                ot[r] = work.tile([P, RUN, nh, QK], F32, name="ot", tag="ot", bufs=OT_BUFS)
             return ot[r]
 
         def rope_mults(k):
@@ -299,10 +305,11 @@ def tile_multilatentattention_pb_kernel(tc, hidden_states, rope_cos, rope_sin, W
                     op=ALU.add,
                 )
 
-        def nope_out(k):
+        def nope_out(k, on_vector=False):
             r, u = k // RUN, k % RUN
             nh = groups[k // MT][1]
-            nc.scalar.copy(out=out_tile(r)[:, u, :, 0:NOPE], in_=acc_n[k].rearrange("p (h d) -> p h d", h=nh))
+            eng_copy = nc.vector.tensor_copy if on_vector else nc.scalar.copy
+            eng_copy(out=out_tile(r)[:, u, :, 0:NOPE], in_=acc_n[k].rearrange("p (h d) -> p h d", h=nh))
 
         def store(k):
             j, m = k // MT, k % MT
@@ -310,31 +317,39 @@ def tile_multilatentattention_pb_kernel(tc, hidden_states, rope_cos, rope_sin, W
             nc.sync.dma_start(out=out_v[m][:, h0 * QK : (h0 + nh) * QK], in_=ot[k // RUN][:, k % RUN, :, :].rearrange("p h d -> p (h d)"))
 
         n_runs = n // RUN
+
+        def pass_from(k):
+            if RUN == 2:
+                return k + ROPE_LAG - 3
+            return ((k - MT) // RUN) * RUN + ROPE_LAG + 1 + max(0, k % MT - 1)
+
         last_step = n + ROPE_LAG + 2 * RUN + 2
         for s in range(last_step):
             if s < n:
-                for t in range(PACK):
-                    widen(s, t, t >= PACK - V_PLANES[s])
+                for t in range(PACK - V_PLANES[s]):
+                    widen(s, t, False)
+            for c in range(0 if s == 0 else s + VW_AHEAD, min(n, s + VW_AHEAD + 1)):
+                for t in range(PACK - V_PLANES[c], PACK):
+                    widen(c, t, True)
             c = s - 1
             if ROPE_PE_FROM <= c < n:
                 ident_rope(c)
             if PE_FROM <= c < n:
                 ident_nope(c)
-            c = s - EVAC_LAG
-            if ROPE_PE_FROM <= c < n:
-                evac_rope(c)
-            if PE_FROM <= c < n:
-                evac_nope(c)
             m = s - 1 - HS_STEP
             if 0 <= m < MT:
                 hs_copy(m, 0)
                 hs_copy(m, 1)
             c = s - 1
             if 0 <= c < n:
-                if c < ROPE_PE_FROM:
-                    inter_v(c, NOPE, QK, grp_r, "grp_r", 3)
+                inter_v(c, NOPE, QK, grp_r, "grp_r", GRPR_BUFS, 1 if c >= ROPE_PE_FROM else 0)
                 if c < PE_FROM:
                     inter_v(c, 0, NOPE, grp_n, "grp_n", 4)
+            c = s - EVAC_LAG
+            if PE_FROM <= c < n:
+                evac_nope(c)
+            if ROPE_PE_FROM <= c < n:
+                evac_rope(c)
             if s == TABLE_STEP:
                 tables()
             c = s - 1 - EVAC_LAG
@@ -346,15 +361,18 @@ def tile_multilatentattention_pb_kernel(tc, hidden_states, rope_cos, rope_sin, W
                 rows = RUN * groups[k0 // MT][1]
                 if r > 0:
                     prows = RUN * groups[(k0 - RUN) // MT][1]
-                    grows = prows * G_ROWS // 16
+                    grows = prows * (G_ROWS if groups[(k0 - RUN) // MT][1] == 4 else G_ROWS_SMALL) // 16
                     rope_add(r - 1, nc.vector, grows, prows)
                     nc.gpsimd.tensor_copy(out=gate[:], in_=ot[r - 1][:, RUN - 1, groups[(k0 - RUN) // MT][1] - 1, QK - 1 : QK])
                     rope_add(r - 1, nc.gpsimd, 0, grows)
+                    if NOUT_ON_V:
+                        for u in range(RUN):
+                            nope_out(k0 - RUN + u, True)
                 for u in range(RUN):
                     rope_mults(k0 + u)
                 if r == n_runs - 1:
                     rope_add(r, nc.vector, 0, rows)
-            c = s - 1
+            c = s - QR_LAG
             if 0 <= c < n:
                 quant(c, True)
             m = s - 1 - HS_STEP
@@ -365,20 +383,20 @@ def tile_multilatentattention_pb_kernel(tc, hidden_states, rope_cos, rope_sin, W
                 hs_transposes(m)
             for k in range(n):
                 for g in range(G):
-                    if max((k // MT) * G + g + 2, k + 3, (k + 2 + HS_STEP) if k < MT else 0) == s:
+                    if max((k // MT) * G + g + PASS_LAG, pass_from(k), (k + 2 + HS_STEP) if k < MT else 0) == s:
                         mm_pass(k, True, g)
             for k in range(n):
                 j, m = k // MT, k % MT
-                if j * G + 6 + m // 2 == s:
+                if j * G + 5 + EVAC_LAG + m // 2 == s:
                     for g in range(G):
                         mm_pass(k, False, g)
             for k in range(n):
                 j, m = k // MT, k % MT
-                if j * G + 6 + m // 2 + NOUT_LAG == s:
+                if j * G + 5 + EVAC_LAG + m // 2 + NOUT_LAG == s and (not NOUT_ON_V or k >= n - RUN):
                     nope_out(k)
             for k in range(n):
                 r = k // RUN
                 j, m = k // MT, k % MT
                 add_step = (r + 1) * RUN + ROPE_LAG if r < n_runs - 1 else r * RUN + ROPE_LAG
-                if max(add_step, j * G + 6 + m // 2 + NOUT_LAG) == s:
+                if max(add_step, j * G + 5 + EVAC_LAG + m // 2 + NOUT_LAG) == s:
                     store(k)

@@ -43,7 +43,13 @@ OT_BUFS = 5
 GRPR_BUFS = 3
 QR_LAG = 1
 NOUT_ON_V = False
+C_PLANES = (0,) * 20
+CAST_BUFS = 6
+S_INTER_FROM = 18
+LAST_NO_G = 1
+S_INTER_HEADS = 1
 G_ROWS_SMALL = 8
+G_ROWS_BY_WINDOW = {4: 5, 2: 2}
 
 
 def tile_multilatentattention_pb_kernel(tc, hidden_states, rope_cos, rope_sin, Wq_bytes, Wq_scale, out):
@@ -94,6 +100,7 @@ def tile_multilatentattention_pb_kernel(tc, hidden_states, rope_cos, rope_sin, W
         grp_r = {}
         grp_n = {}
         pis = {}
+        casts = {}
         pir = {}
         wc = {}
         xts = {}
@@ -152,9 +159,29 @@ def tile_multilatentattention_pb_kernel(tc, hidden_states, rope_cos, rope_sin, W
             else:
                 nc.scalar.activation(out=dst, in_=src, func=ACT.Copy, scale=sc[:, g, t : t + 1])
 
+        def cast_plane(c, t):
+            nh = heads_of(c)
+            casts[(c, t)] = work.tile([P, nh * QK], BF16, name="cast", tag="cast", bufs=CAST_BUFS)
+            nc.scalar.copy(out=casts[(c, t)][:], in_=wb[c][t].bitcast(FP8))
+
+        def scale_plane(c, t):
+            nc.vector.tensor_scalar(out=planes[c][:, t, :], in0=casts[(c, t)][:], scalar1=sc[:, c % G, t : t + 1], scalar2=None, op0=ALU.mult)
+
+        def inter_s(c, heads):
+            nh = heads_of(c)
+            grp_r[c] = work.tile([P, nh * ROPE * PACK], BF16, name="grp_r", tag="grp_r", bufs=GRPR_BUFS, align_bytes=64)
+            for h in range(nh - heads, nh):
+                nc.scalar.copy(
+                    out=grp_r[c][:].rearrange("p (h c i t) -> p h c t i", h=nh, i=4, t=PACK)[:, h],
+                    in_=planes[c][:].rearrange("p t (h d) -> p t h d", d=QK)[:, :, h, NOPE:QK].rearrange("p t (c i) -> p c t i", i=4),
+                )
+
         def inter_v(c, lo, hi, store, tag, bufs, skip=0):
             nh = heads_of(c)
-            store[c] = work.tile([P, nh * (hi - lo) * PACK], BF16, name=tag, tag=tag, bufs=bufs, align_bytes=64)
+            if c not in store:
+                store[c] = work.tile([P, nh * (hi - lo) * PACK], BF16, name=tag, tag=tag, bufs=bufs, align_bytes=64)
+            if skip == nh:
+                return
             nc.vector.tensor_copy(
                 out=store[c][:].rearrange("p (h c i t) -> p h c t i", h=nh, i=4, t=PACK)[:, 0 : nh - skip],
                 in_=planes[c][:].rearrange("p t (h d) -> p t h d", d=QK)[:, :, 0 : nh - skip, lo:hi].rearrange("p t h (c i) -> p h c t i", i=4),
@@ -326,8 +353,14 @@ def tile_multilatentattention_pb_kernel(tc, hidden_states, rope_cos, rope_sin, W
         last_step = n + ROPE_LAG + 2 * RUN + 2
         for s in range(last_step):
             if s < n:
-                for t in range(PACK - V_PLANES[s]):
+                for t in range(C_PLANES[s]):
+                    cast_plane(s, t)
+                for t in range(C_PLANES[s], PACK - V_PLANES[s]):
                     widen(s, t, False)
+                for t in range(C_PLANES[s]):
+                    scale_plane(s, t)
+                if s >= S_INTER_FROM:
+                    inter_s(s, S_INTER_HEADS)
             for c in range(0 if s == 0 else s + VW_AHEAD, min(n, s + VW_AHEAD + 1)):
                 for t in range(PACK - V_PLANES[c], PACK):
                     widen(c, t, True)
@@ -342,7 +375,7 @@ def tile_multilatentattention_pb_kernel(tc, hidden_states, rope_cos, rope_sin, W
                 hs_copy(m, 1)
             c = s - 1
             if 0 <= c < n:
-                inter_v(c, NOPE, QK, grp_r, "grp_r", GRPR_BUFS, 1 if c >= ROPE_PE_FROM else 0)
+                inter_v(c, NOPE, QK, grp_r, "grp_r", GRPR_BUFS, 1 if c >= ROPE_PE_FROM else (S_INTER_HEADS if c >= S_INTER_FROM else 0))
                 if c < PE_FROM:
                     inter_v(c, 0, NOPE, grp_n, "grp_n", 4)
             c = s - EVAC_LAG
@@ -361,10 +394,13 @@ def tile_multilatentattention_pb_kernel(tc, hidden_states, rope_cos, rope_sin, W
                 rows = RUN * groups[k0 // MT][1]
                 if r > 0:
                     prows = RUN * groups[(k0 - RUN) // MT][1]
-                    grows = prows * (G_ROWS if groups[(k0 - RUN) // MT][1] == 4 else G_ROWS_SMALL) // 16
+                    grows = min(prows - 1, G_ROWS_BY_WINDOW[groups[k0 // MT][1]])
+                    if r >= n_runs - LAST_NO_G:
+                        grows = 0
                     rope_add(r - 1, nc.vector, grows, prows)
-                    nc.gpsimd.tensor_copy(out=gate[:], in_=ot[r - 1][:, RUN - 1, groups[(k0 - RUN) // MT][1] - 1, QK - 1 : QK])
-                    rope_add(r - 1, nc.gpsimd, 0, grows)
+                    if grows > 0:
+                        nc.gpsimd.tensor_copy(out=gate[:], in_=ot[r - 1][:, RUN - 1, groups[(k0 - RUN) // MT][1] - 1, QK - 1 : QK])
+                        rope_add(r - 1, nc.gpsimd, 0, grows)
                     if NOUT_ON_V:
                         for u in range(RUN):
                             nope_out(k0 - RUN + u, True)

@@ -39,14 +39,16 @@ HS_STEP = 1
 PASS_LAG = 2
 VW_AHEAD = 0
 PLANE_BUFS = 4
-OT_BUFS = 5
-GRPR_BUFS = 3
+OT_BUFS = 4
+GRPR_BUFS = 2
 QR_LAG = 1
 NOUT_ON_V = False
 C_PLANES = (0,) * 20
 CAST_BUFS = 6
 S_INTER_FROM = 18
 LAST_NO_G = 1
+MERGE_R_UNTIL = 20
+FIRST_PLANES = (2, 0, 3, 1)
 S_INTER_HEADS = 1
 G_ROWS_SMALL = 8
 G_ROWS_BY_WINDOW = {4: 5, 2: 2}
@@ -83,13 +85,15 @@ def tile_multilatentattention_pb_kernel(tc, hidden_states, rope_cos, rope_sin, W
         warm_i = const.tile([P, 1], F32, name="warm_i")
         warm_o = const.tile([P, 1], F32, name="warm_o")
         gate = const.tile([P, 1], F32, name="gate")
+        sign = const.tile([P, 2], F32, name="sign")
         nc.vector.memset(warm_i[:], 0.0)
+        nc.vector.memset(sign[:, 0:1], -1.0)
+        nc.vector.memset(sign[:, 1:2], 1.0)
         nc.scalar.activation(out=warm_o[:], in_=warm_i[:], func=ACT.Copy)
 
         sc = const.tile([P, G, PACK], F32, name="sc")
         cos_sb = const.tile([P, MT, HALF], BF16, name="cos_sb")
         sin_sb = const.tile([P, MT, HALF], BF16, name="sin_sb")
-        c2 = const.tile([P, MT, ROPE], F32, name="c2")
         s2 = const.tile([P, MT, ROPE], F32, name="s2")
         hs_codes = const.tile([P, MT, G * P], U32, name="hs_codes", align_bytes=64)
         hs_scales = const.tile([P, MT, G * P], U8, name="hs_scales", align_bytes=64)
@@ -119,11 +123,11 @@ def tile_multilatentattention_pb_kernel(tc, hidden_states, rope_cos, rope_sin, W
             h0, nh = groups[j]
             cols = slice(h0 * QK, (h0 + nh) * QK)
             if c == 0:
-                wb[c] = []
-                for t in range(PACK):
+                wb[c] = [None] * PACK
+                for t in FIRST_PLANES:
                     one = const.tile([P, nh * QK], U8, name="wq_bytes_%d_%d" % (c, t))
                     nc.sync.dma_start(out=one[:], in_=w_v[g][:, t, cols])
-                    wb[c].append(one[:])
+                    wb[c][t] = one[:]
             else:
                 whole = const.tile([P, PACK, nh * QK], U8, name="wq_bytes_%d" % c)
                 nc.sync.dma_start(out=whole[:], in_=w_v[g][:, :, cols])
@@ -169,22 +173,17 @@ def tile_multilatentattention_pb_kernel(tc, hidden_states, rope_cos, rope_sin, W
 
         def inter_s(c, heads):
             nh = heads_of(c)
-            grp_r[c] = work.tile([P, nh * ROPE * PACK], BF16, name="grp_r", tag="grp_r", bufs=GRPR_BUFS, align_bytes=64)
             for h in range(nh - heads, nh):
                 nc.scalar.copy(
-                    out=grp_r[c][:].rearrange("p (h c i t) -> p h c t i", h=nh, i=4, t=PACK)[:, h],
+                    out=rope_part(c).rearrange("p (h c i t) -> p h c t i", h=nh, i=4, t=PACK)[:, h],
                     in_=planes[c][:].rearrange("p t (h d) -> p t h d", d=QK)[:, :, h, NOPE:QK].rearrange("p t (c i) -> p c t i", i=4),
                 )
 
-        def inter_v(c, lo, hi, store, tag, bufs, skip=0):
+        def inter_rope_v(c, skip):
             nh = heads_of(c)
-            if c not in store:
-                store[c] = work.tile([P, nh * (hi - lo) * PACK], BF16, name=tag, tag=tag, bufs=bufs, align_bytes=64)
-            if skip == nh:
-                return
             nc.vector.tensor_copy(
-                out=store[c][:].rearrange("p (h c i t) -> p h c t i", h=nh, i=4, t=PACK)[:, 0 : nh - skip],
-                in_=planes[c][:].rearrange("p t (h d) -> p t h d", d=QK)[:, :, 0 : nh - skip, lo:hi].rearrange("p t h (c i) -> p h c t i", i=4),
+                out=rope_part(c).rearrange("p (h c i t) -> p h c t i", h=nh, i=4, t=PACK)[:, 0 : nh - skip],
+                in_=planes[c][:].rearrange("p t (h d) -> p t h d", d=QK)[:, :, 0 : nh - skip, NOPE:QK].rearrange("p t h (c i) -> p h c t i", i=4),
             )
 
         def ident_nope(c):
@@ -200,26 +199,27 @@ def tile_multilatentattention_pb_kernel(tc, hidden_states, rope_cos, rope_sin, W
                     stop=True,
                 )
 
-        def evac_nope(c):
-            nh = heads_of(c)
-            grp_n[c] = work.tile([P, nh * NOPE * PACK], BF16, name="grp_n", tag="grp_n", bufs=4, align_bytes=64)
-            nc.scalar.copy(out=grp_n[c][:], in_=pis[c][:])
+        def nope_part(c):
+            j = c // G
+            if j not in grp_n:
+                grp_n[j] = work.tile([P, G, groups[j][1] * NOPE * PACK], BF16, name="grp_n", tag="grp_n", bufs=2, align_bytes=64)
+            return grp_n[j][:, c % G, :]
 
-        def ident_rope(c):
+        def evac_nope(c):
+            nc.scalar.copy(out=nope_part(c), in_=pis[c][:])
+
+        def inter_nope_v(c):
             nh = heads_of(c)
-            src = planes[c][:].rearrange("p t (h d) -> p h d t", d=QK)[:, :, NOPE:QK, :]
-            pir[c] = ps.tile([P, ROPE * PACK], BF16, name="pir", tag="misc", bufs=2)
-            nc.tensor.matmul(
-                out=pir[c][:].rearrange("p (d t) -> p d t", t=PACK),
-                lhsT=ident_b[:],
-                rhs=src[:, nh - 1, :, :],
-                start=True,
-                stop=True,
+            nc.vector.tensor_copy(
+                out=nope_part(c).rearrange("p (h c i t) -> p h c t i", h=nh, i=4, t=PACK),
+                in_=planes[c][:].rearrange("p t (h d) -> p t h d", d=QK)[:, :, :, 0:NOPE].rearrange("p t h (c i) -> p h c t i", i=4),
             )
 
-        def evac_rope(c):
-            nh = heads_of(c)
-            nc.scalar.copy(out=grp_r[c][:, (nh - 1) * ROPE * PACK :], in_=pir[c][:])
+        def rope_part(c):
+            q = c // 2
+            if q not in grp_r:
+                grp_r[q] = work.tile([P, 2, heads_of(c) * ROPE * PACK], BF16, name="grp_r", tag="grp_r", bufs=GRPR_BUFS, align_bytes=64)
+            return grp_r[q][:, c % 2, :]
 
         def codes_of(j):
             if j not in wc:
@@ -232,13 +232,25 @@ def tile_multilatentattention_pb_kernel(tc, hidden_states, rope_cos, rope_sin, W
                 )
             return wc[j]
 
-        def quant(c, rope):
+        def quant_rope(c, both):
             j, g = c // G, c % G
             t = codes_of(j)
-            if rope:
-                nc.vector.quantize_mx(out=t[0][:, g, :].bitcast(FP8X4), scales=t[1][:, g, :], in_=grp_r[c][:])
+            if both:
+                nc.vector.quantize_mx(
+                    out=t[0][:, g - 1 : g + 1, :].rearrange("p g x -> p (g x)").bitcast(FP8X4),
+                    scales=t[1][:, g - 1 : g + 1, :].rearrange("p g x -> p (g x)"),
+                    in_=grp_r[c // 2][:].rearrange("p g x -> p (g x)"),
+                )
             else:
-                nc.vector.quantize_mx(out=t[2][:, g, :].bitcast(FP8X4), scales=t[3][:, g, :], in_=grp_n[c][:])
+                nc.vector.quantize_mx(out=t[0][:, g, :].bitcast(FP8X4), scales=t[1][:, g, :], in_=rope_part(c))
+
+        def quant_nope(j):
+            t = codes_of(j)
+            nc.vector.quantize_mx(
+                out=t[2][:].rearrange("p g x -> p (g x)").bitcast(FP8X4),
+                scales=t[3][:].rearrange("p g x -> p (g x)"),
+                in_=grp_n[j][:].rearrange("p g x -> p (g x)"),
+            )
 
         def hs_transposes(m):
             words = hs_raw[m][:].bitcast(F32)
@@ -262,13 +274,12 @@ def tile_multilatentattention_pb_kernel(tc, hidden_states, rope_cos, rope_sin, W
             nc.vector.quantize_mx(out=hs_codes[:, m, :].bitcast(FP8X4), scales=hs_scales[:, m, :], in_=hs_grp[m][:])
 
         def tables():
-            cq = cos_sb[:].rearrange("p m i -> p (m i)").unsqueeze(2)
-            sq = sin_sb[:].rearrange("p m i -> p (m i)").unsqueeze(2)
-            c2v = c2[:].rearrange("p m (i e) -> p (m i) e", e=2)
-            s2v = s2[:].rearrange("p m (i e) -> p (m i) e", e=2)
-            nc.vector.tensor_copy(out=c2v, in_=cq.to_broadcast([P, MT * HALF, 2]))
-            nc.vector.tensor_scalar(out=s2v[:, :, 0:1], in0=sq, scalar1=-1.0, scalar2=None, op0=ALU.mult)
-            nc.vector.tensor_copy(out=s2v[:, :, 1:2], in_=sq)
+            nc.vector.tensor_tensor(
+                out=s2[:].rearrange("p m (i e) -> p (m i) e", e=2),
+                in0=sin_sb[:].rearrange("p m i -> p (m i)").unsqueeze(2).to_broadcast([P, MT * HALF, 2]),
+                in1=sign[:].unsqueeze(1).to_broadcast([P, MT * HALF, 2]),
+                op=ALU.mult,
+            )
 
         def mm_pass(k, rope, g):
             j, m = k // MT, k % MT
@@ -311,9 +322,9 @@ def tile_multilatentattention_pb_kernel(tc, hidden_states, rope_cos, rope_sin, W
             r, u, m = k // RUN, k % RUN, k % MT
             nh = run_tiles(r)
             nc.vector.tensor_tensor(
-                out=ta[r][:, u, :, :],
-                in0=acc_r[k][:].rearrange("p (h d) -> p h d", h=nh),
-                in1=c2[:, m, :].unsqueeze(1).to_broadcast([P, nh, ROPE]),
+                out=ta[r][:, u, :, :].rearrange("p h (i e) -> p h i e", e=2),
+                in0=acc_r[k][:].rearrange("p (h i e) -> p h i e", h=nh, e=2),
+                in1=cos_sb[:, m, :].unsqueeze(1).unsqueeze(3).to_broadcast([P, nh, HALF, 2]),
                 op=ALU.mult,
             )
             nc.vector.tensor_tensor(
@@ -345,6 +356,9 @@ def tile_multilatentattention_pb_kernel(tc, hidden_states, rope_cos, rope_sin, W
 
         n_runs = n // RUN
 
+        def quant_chunk(c):
+            return c if c >= MERGE_R_UNTIL else c + 1 - c % 2
+
         def pass_from(k):
             if RUN == 2:
                 return k + ROPE_LAG - 3
@@ -365,8 +379,6 @@ def tile_multilatentattention_pb_kernel(tc, hidden_states, rope_cos, rope_sin, W
                 for t in range(PACK - V_PLANES[c], PACK):
                     widen(c, t, True)
             c = s - 1
-            if ROPE_PE_FROM <= c < n:
-                ident_rope(c)
             if PE_FROM <= c < n:
                 ident_nope(c)
             m = s - 1 - HS_STEP
@@ -375,19 +387,17 @@ def tile_multilatentattention_pb_kernel(tc, hidden_states, rope_cos, rope_sin, W
                 hs_copy(m, 1)
             c = s - 1
             if 0 <= c < n:
-                inter_v(c, NOPE, QK, grp_r, "grp_r", GRPR_BUFS, 1 if c >= ROPE_PE_FROM else (S_INTER_HEADS if c >= S_INTER_FROM else 0))
+                inter_rope_v(c, S_INTER_HEADS if c >= S_INTER_FROM else 0)
                 if c < PE_FROM:
-                    inter_v(c, 0, NOPE, grp_n, "grp_n", 4)
+                    inter_nope_v(c)
             c = s - EVAC_LAG
             if PE_FROM <= c < n:
                 evac_nope(c)
-            if ROPE_PE_FROM <= c < n:
-                evac_rope(c)
             if s == TABLE_STEP:
                 tables()
             c = s - 1 - EVAC_LAG
-            if 0 <= c < n:
-                quant(c, False)
+            if 0 <= c < n and c % G == G - 1:
+                quant_nope(c // G)
             k0 = s - ROPE_LAG
             if k0 >= 0 and k0 % RUN == 0 and k0 < n:
                 r = k0 // RUN
@@ -407,10 +417,14 @@ def tile_multilatentattention_pb_kernel(tc, hidden_states, rope_cos, rope_sin, W
                 for u in range(RUN):
                     rope_mults(k0 + u)
                 if r == n_runs - 1:
-                    rope_add(r, nc.vector, 0, rows)
+                    for u in range(RUN):
+                        rope_add(r, nc.vector, u * rows // RUN, (u + 1) * rows // RUN)
             c = s - QR_LAG
             if 0 <= c < n:
-                quant(c, True)
+                if c >= MERGE_R_UNTIL:
+                    quant_rope(c, False)
+                elif c % 2 == 1:
+                    quant_rope(c, True)
             m = s - 1 - HS_STEP
             if 0 <= m < MT:
                 hs_quant(m)
@@ -419,7 +433,7 @@ def tile_multilatentattention_pb_kernel(tc, hidden_states, rope_cos, rope_sin, W
                 hs_transposes(m)
             for k in range(n):
                 for g in range(G):
-                    if max((k // MT) * G + g + PASS_LAG, pass_from(k), (k + 2 + HS_STEP) if k < MT else 0) == s:
+                    if max(quant_chunk((k // MT) * G + g) + PASS_LAG, pass_from(k), (k + 2 + HS_STEP) if k < MT else 0) == s:
                         mm_pass(k, True, g)
             for k in range(n):
                 j, m = k // MT, k % MT

@@ -25,7 +25,7 @@ FLOPS = 2 * T * HID * H * QK
 
 GROUP_HEADS = (4, 4, 4, 2, 2)
 RUN = 2
-V_PLANES = (2, 2, 2, 2, 1, 0, 1, 0, 1, 0, 0, 0, 0, 0, 0, 0, 0, 0, 0, 0)
+V_PLANES = (2, 2, 2, 2, 1, 1, 1, 1, 1, 1, 0, 0, 0, 0, 0, 0, 0, 0, 0, 0)
 PE_FROM = 4
 ROPE_PE_FROM = 20
 G_ROWS = 10
@@ -48,7 +48,7 @@ CAST_BUFS = 6
 S_INTER_FROM = 18
 LAST_NO_G = 1
 MERGE_R_UNTIL = 20
-FIRST_PLANES = (2, 0, 3, 1)
+FIRST_PLANES = (0, 1, 2, 3)
 S_INTER_HEADS = 1
 G_ROWS_SMALL = 8
 G_ROWS_BY_WINDOW = {4: 5, 2: 2}

@@ -32,10 +32,10 @@ G_ROWS = 10
 EVAC_LAG = 2
 ROPE_LAG = 6
 HS_ON_S = (0, 1)
-LOAD_ORDER = ("w0", "w1", "h0", "cs", "w2", "h1", "w3", "h2", "w4", "h3")
-TABLE_STEP = 3
+LOAD_ORDER = ("w0", "w1", "w2", "h0", "w3", "h1", "cs", "w4", "h2", "w5", "h3")
+TABLE_STEP = 4
 NOUT_LAG = 1
-HS_STEP = 1
+HS_STEP = 2
 PASS_LAG = 2
 VW_AHEAD = 0
 PLANE_BUFS = 4

@@ -25,7 +25,7 @@ FLOPS = 2 * T * HID * H * QK
 
 GROUP_HEADS = (4, 4, 4, 2, 2)
 RUN = 2
-V_PLANES = (2, 2, 2, 2, 1, 1, 1, 1, 1, 1, 0, 0, 0, 0, 0, 0, 0, 0, 0, 0)
+V_PLANES = (2, 2, 2, 2, 1, 1, 1, 0, 1, 0, 0, 0, 0, 0, 0, 0, 0, 0, 0, 0)
 PE_FROM = 4
 ROPE_PE_FROM = 20
 G_ROWS = 10
@@ -34,7 +34,7 @@ ROPE_LAG = 6
 HS_ON_S = (0, 1)
 LOAD_ORDER = ("w0", "w1", "w2", "h0", "w3", "h1", "cs", "w4", "h2", "w5", "h3")
 TABLE_STEP = 4
-NOUT_LAG = 1
+NOUT_LAG = 2
 HS_STEP = 2
 PASS_LAG = 2
 VW_AHEAD = 0
@@ -111,6 +111,7 @@ def tile_multilatentattention_pb_kernel(tc, hidden_states, rope_cos, rope_sin, W
         hs_grp = {}
         acc_r = {}
         acc_n = {}
+        acc_pair = {}
         ta = {}
         tb = {}
         ot = {}
@@ -294,6 +295,7 @@ def tile_multilatentattention_pb_kernel(tc, hidden_states, rope_cos, rope_sin, W
                     pair = ps.tile([P, 2, nh * NOPE], F32, name="acc_n", tag="acc_n", bufs=2)
                     acc_n[k] = pair[:, 0, :]
                     acc_n[k + 1] = pair[:, 1, :]
+                    acc_pair[k] = pair
                 acc, cod, sca = acc_n[k], t[2], t[3]
             nc.tensor.matmul_mx(
                 out=acc,
@@ -348,6 +350,10 @@ def tile_multilatentattention_pb_kernel(tc, hidden_states, rope_cos, rope_sin, W
             nh = groups[k // MT][1]
             eng_copy = nc.vector.tensor_copy if on_vector else nc.scalar.copy
             eng_copy(out=out_tile(r)[:, u, :, 0:NOPE], in_=acc_n[k].rearrange("p (h d) -> p h d", h=nh))
+
+        def nope_out_pair(k):
+            nh = groups[k // MT][1]
+            nc.scalar.copy(out=out_tile(k // RUN)[:, :, :, 0:NOPE], in_=acc_pair[k][:].rearrange("p u (h d) -> p u h d", h=nh))
 
         def store(k):
             j, m = k // MT, k % MT
@@ -442,8 +448,8 @@ def tile_multilatentattention_pb_kernel(tc, hidden_states, rope_cos, rope_sin, W
                         mm_pass(k, False, g)
             for k in range(n):
                 j, m = k // MT, k % MT
-                if j * G + 5 + EVAC_LAG + m // 2 + NOUT_LAG == s and (not NOUT_ON_V or k >= n - RUN):
-                    nope_out(k)
+                if j * G + 5 + EVAC_LAG + m // 2 + NOUT_LAG == s and k % 2 == 0:
+                    nope_out_pair(k)
             for k in range(n):
                 r = k // RUN
                 j, m = k // MT, k % MT

@@ -34,11 +34,11 @@ ROPE_LAG = 6
 HS_ON_S = (0, 1)
 LOAD_ORDER = ("w0", "w1", "w2", "h0", "w3", "h1", "cs", "w4", "h2", "w5", "h3")
 TABLE_STEP = 4
-NOUT_LAG = 2
+NOUT_LAG = 3
 HS_STEP = 2
 PASS_LAG = 2
 VW_AHEAD = 0
-PLANE_BUFS = 4
+PLANE_BUFS = 5
 OT_BUFS = 4
 GRPR_BUFS = 2
 QR_LAG = 1

@@ -24,34 +24,30 @@ MT = T // P
 FLOPS = 2 * T * HID * H * QK
 
 GROUP_HEADS = (4, 4, 4, 2, 2)
-RUN = 2
+N_CHUNKS = 20
+RUN_UNITS = (2,) * 10
 V_PLANES = (2, 2, 2, 2, 1, 1, 1, 0, 1, 0, 0, 0, 0, 0, 0, 0, 0, 0, 0, 0)
 PE_FROM = 4
-ROPE_PE_FROM = 20
-G_ROWS = 10
+PE_ROPE = ()
 EVAC_LAG = 2
-ROPE_LAG = 6
-HS_ON_S = (0, 1)
+HS_STEP = 2
 LOAD_ORDER = ("w0", "w1", "w2", "h0", "w3", "h1", "cs", "w4", "h2", "w5", "h3")
 TABLE_STEP = 4
-NOUT_LAG = 3
-HS_STEP = 2
-PASS_LAG = 2
-VW_AHEAD = 0
 PLANE_BUFS = 5
 OT_BUFS = 4
+TAB_BUFS = 3
+WC_BUFS = 2
 GRPR_BUFS = 2
-QR_LAG = 1
-NOUT_ON_V = False
-C_PLANES = (0,) * 20
-CAST_BUFS = 6
-S_INTER_FROM = 18
-LAST_NO_G = 1
-MERGE_R_UNTIL = 20
-FIRST_PLANES = (0, 1, 2, 3)
-S_INTER_HEADS = 1
-G_ROWS_SMALL = 8
-G_ROWS_BY_WINDOW = {4: 5, 2: 2}
+S_INTER = {18: 1, 19: 1}
+WIN_STEP = tuple(range(6, 26, 2))
+PASS_STEP = {}
+NOPE_STEP = (7, 11, 15, 19, 23)
+NOUT_LAG = 3
+LEFT_G = (0, 6, 6, 6, 6, 6, 2, 2, 2, 0)
+OWN_G = (0,) * 10
+GATE = "early"
+MERGE_UNTIL = 20
+SPLIT_LAST = True
 
 
 def tile_multilatentattention_pb_kernel(tc, hidden_states, rope_cos, rope_sin, Wq_bytes, Wq_scale, out):
@@ -68,7 +64,12 @@ def tile_multilatentattention_pb_kernel(tc, hidden_states, rope_cos, rope_sin, W
     for heads in GROUP_HEADS:
         groups.append((first, heads))
         first += heads
-    n = len(groups) * G
+    n = N_CHUNKS
+    runs = []
+    first = 0
+    for units in RUN_UNITS:
+        runs.append(list(range(first, first + units)))
+        first += units
 
     with ExitStack() as ctx:
         const = ctx.enter_context(tc.tile_pool(name="const", bufs=1))
@@ -104,8 +105,6 @@ def tile_multilatentattention_pb_kernel(tc, hidden_states, rope_cos, rope_sin, W
         grp_r = {}
         grp_n = {}
         pis = {}
-        casts = {}
-        pir = {}
         wc = {}
         xts = {}
         hs_grp = {}
@@ -125,7 +124,7 @@ def tile_multilatentattention_pb_kernel(tc, hidden_states, rope_cos, rope_sin, W
             cols = slice(h0 * QK, (h0 + nh) * QK)
             if c == 0:
                 wb[c] = [None] * PACK
-                for t in FIRST_PLANES:
+                for t in range(PACK):
                     one = const.tile([P, nh * QK], U8, name="wq_bytes_%d_%d" % (c, t))
                     nc.sync.dma_start(out=one[:], in_=w_v[g][:, t, cols])
                     wb[c][t] = one[:]
@@ -164,14 +163,6 @@ def tile_multilatentattention_pb_kernel(tc, hidden_states, rope_cos, rope_sin, W
             else:
                 nc.scalar.activation(out=dst, in_=src, func=ACT.Copy, scale=sc[:, g, t : t + 1])
 
-        def cast_plane(c, t):
-            nh = heads_of(c)
-            casts[(c, t)] = work.tile([P, nh * QK], BF16, name="cast", tag="cast", bufs=CAST_BUFS)
-            nc.scalar.copy(out=casts[(c, t)][:], in_=wb[c][t].bitcast(FP8))
-
-        def scale_plane(c, t):
-            nc.vector.tensor_scalar(out=planes[c][:, t, :], in0=casts[(c, t)][:], scalar1=sc[:, c % G, t : t + 1], scalar2=None, op0=ALU.mult)
-
         def inter_s(c, heads):
             nh = heads_of(c)
             for h in range(nh - heads, nh):
@@ -182,20 +173,31 @@ def tile_multilatentattention_pb_kernel(tc, hidden_states, rope_cos, rope_sin, W
 
         def inter_rope_v(c, skip):
             nh = heads_of(c)
+            if skip == nh:
+                return
             nc.vector.tensor_copy(
                 out=rope_part(c).rearrange("p (h c i t) -> p h c t i", h=nh, i=4, t=PACK)[:, 0 : nh - skip],
                 in_=planes[c][:].rearrange("p t (h d) -> p t h d", d=QK)[:, :, 0 : nh - skip, NOPE:QK].rearrange("p t h (c i) -> p h c t i", i=4),
             )
 
-        def ident_nope(c):
+        def ident_chunk(c):
             nh = heads_of(c)
-            src = planes[c][:].rearrange("p t (h d) -> p h d t", d=QK)[:, :, 0:NOPE, :]
-            pis[c] = ps.tile([P, nh * NOPE * PACK], BF16, name="pi", tag="misc", bufs=2)
+            view = planes[c][:].rearrange("p t (h d) -> p h d t", d=QK)
+            rope_head = 1 if c in PE_ROPE else 0
+            pis[c] = ps.tile([P, nh * NOPE * PACK + rope_head * ROPE * PACK], BF16, name="pi", tag="misc", bufs=2)
             for a in range(nh // 2):
                 nc.tensor.matmul(
                     out=pis[c][:, a * 512 : (a + 1) * 512].rearrange("p (h d t) -> p h d t", h=2, t=PACK),
                     lhsT=ident_b[:],
-                    rhs=src[:, 2 * a : 2 * a + 2, :, :],
+                    rhs=view[:, 2 * a : 2 * a + 2, 0:NOPE, :],
+                    start=True,
+                    stop=True,
+                )
+            if rope_head:
+                nc.tensor.matmul(
+                    out=pis[c][:, nh * 256 : nh * 256 + 512].rearrange("p (d t) -> p d t", t=PACK),
+                    lhsT=ident_b[:],
+                    rhs=view[:, nh - 1, NOPE:QK, :],
                     start=True,
                     stop=True,
                 )
@@ -206,8 +208,11 @@ def tile_multilatentattention_pb_kernel(tc, hidden_states, rope_cos, rope_sin, W
                 grp_n[j] = work.tile([P, G, groups[j][1] * NOPE * PACK], BF16, name="grp_n", tag="grp_n", bufs=2, align_bytes=64)
             return grp_n[j][:, c % G, :]
 
-        def evac_nope(c):
-            nc.scalar.copy(out=nope_part(c), in_=pis[c][:])
+        def evac_chunk(c):
+            nh = heads_of(c)
+            if c in PE_ROPE:
+                nc.scalar.copy(out=rope_part(c)[:, (nh - 1) * 512 : nh * 512], in_=pis[c][:, nh * 256 : nh * 256 + 512])
+            nc.scalar.copy(out=nope_part(c), in_=pis[c][:, 0 : nh * 256])
 
         def inter_nope_v(c):
             nh = heads_of(c)
@@ -226,10 +231,10 @@ def tile_multilatentattention_pb_kernel(tc, hidden_states, rope_cos, rope_sin, W
             if j not in wc:
                 nh = groups[j][1]
                 wc[j] = (
-                    work.tile([P, G, nh * ROPE], U32, name="wc_r", tag="wc_r", bufs=3, align_bytes=64),
-                    work.tile([P, G, nh * ROPE], U8, name="ws_r", tag="ws_r", bufs=3, align_bytes=64),
-                    work.tile([P, G, nh * NOPE], U32, name="wc_n", tag="wc_n", bufs=3, align_bytes=64),
-                    work.tile([P, G, nh * NOPE], U8, name="ws_n", tag="ws_n", bufs=3, align_bytes=64),
+                    work.tile([P, G, nh * ROPE], U32, name="wc_r", tag="wc_r", bufs=WC_BUFS, align_bytes=64),
+                    work.tile([P, G, nh * ROPE], U8, name="ws_r", tag="ws_r", bufs=WC_BUFS, align_bytes=64),
+                    work.tile([P, G, nh * NOPE], U32, name="wc_n", tag="wc_n", bufs=WC_BUFS, align_bytes=64),
+                    work.tile([P, G, nh * NOPE], U8, name="ws_n", tag="ws_n", bufs=WC_BUFS, align_bytes=64),
                 )
             return wc[j]
 
@@ -268,8 +273,7 @@ def tile_multilatentattention_pb_kernel(tc, hidden_states, rope_cos, rope_sin, W
             if m not in hs_grp:
                 hs_grp[m] = work.tile([P, G * P * PACK], BF16, name="hs_grp", tag="hs_grp", bufs=2, align_bytes=64)
             dst = hs_grp[m][:].bitcast(F32).rearrange("p (g r u) -> p g r u", g=G, u=2)
-            eng_copy = nc.scalar.copy if half in HS_ON_S else nc.vector.tensor_copy
-            eng_copy(out=dst[:, 2 * half : 2 * half + 2, :, :], in_=xts[m][half][:].rearrange("p g u r -> p g r u"))
+            nc.scalar.copy(out=dst[:, 2 * half : 2 * half + 2, :, :], in_=xts[m][half][:].rearrange("p g u r -> p g r u"))
 
         def hs_quant(m):
             nc.vector.quantize_mx(out=hs_codes[:, m, :].bitcast(FP8X4), scales=hs_scales[:, m, :], in_=hs_grp[m][:])
@@ -307,130 +311,160 @@ def tile_multilatentattention_pb_kernel(tc, hidden_states, rope_cos, rope_sin, W
                 stop=(g == G - 1),
             )
 
-        def run_tiles(r):
-            nh = groups[r * RUN // MT][1]
-            if r not in ta:
-                ta[r] = work.tile([P, RUN, nh, ROPE], F32, name="ta", tag="ta", bufs=2)
-                tb[r] = work.tile([P, RUN, nh, ROPE], F32, name="tb", tag="tb", bufs=2)
+        def nh_pair(q):
+            return groups[2 * q // MT][1]
+
+        def pair_tiles(q):
+            nh = nh_pair(q)
+            if q not in ta:
+                ta[q] = work.tile([P, 2, nh, ROPE], F32, name="ta", tag="ta", bufs=TAB_BUFS)
+                tb[q] = work.tile([P, 2, nh, ROPE], F32, name="tb", tag="tb", bufs=TAB_BUFS)
             return nh
 
-        def out_tile(r):
-            nh = groups[r * RUN // MT][1]
-            if r not in ot:
-                ot[r] = work.tile([P, RUN, nh, QK], F32, name="ot", tag="ot", bufs=OT_BUFS)
-            return ot[r]
+        def out_tile(q):
+            if q not in ot:
+                ot[q] = work.tile([P, 2, nh_pair(q), QK], F32, name="ot", tag="ot", bufs=OT_BUFS)
+            return ot[q]
 
         def rope_mults(k):
-            r, u, m = k // RUN, k % RUN, k % MT
-            nh = run_tiles(r)
+            q, u, m = k // 2, k % 2, k % MT
+            nh = pair_tiles(q)
             nc.vector.tensor_tensor(
-                out=ta[r][:, u, :, :].rearrange("p h (i e) -> p h i e", e=2),
+                out=ta[q][:, u, :, :].rearrange("p h (i e) -> p h i e", e=2),
                 in0=acc_r[k][:].rearrange("p (h i e) -> p h i e", h=nh, e=2),
                 in1=cos_sb[:, m, :].unsqueeze(1).unsqueeze(3).to_broadcast([P, nh, HALF, 2]),
                 op=ALU.mult,
             )
             nc.vector.tensor_tensor(
-                out=tb[r][:, u, :, :].rearrange("p h (i e) -> p h i e", e=2),
+                out=tb[q][:, u, :, :].rearrange("p h (i e) -> p h i e", e=2),
                 in0=acc_r[k][:].rearrange("p (h i e) -> p h i e", h=nh, e=2)[:, :, :, ::-1],
                 in1=s2[:, m, :].rearrange("p (i e) -> p i e", e=2).unsqueeze(1).to_broadcast([P, nh, HALF, 2]),
                 op=ALU.mult,
             )
 
-        def rope_add(r, eng, lo, hi):
+        def rope_add(q, eng, lo, hi):
             if hi > lo:
                 eng.tensor_tensor(
-                    out=out_tile(r)[:].rearrange("p u h d -> p (u h) d")[:, lo:hi, NOPE:QK],
-                    in0=ta[r][:].rearrange("p u h d -> p (u h) d")[:, lo:hi, :],
-                    in1=tb[r][:].rearrange("p u h d -> p (u h) d")[:, lo:hi, :],
+                    out=out_tile(q)[:].rearrange("p u h d -> p (u h) d")[:, lo:hi, NOPE:QK],
+                    in0=ta[q][:].rearrange("p u h d -> p (u h) d")[:, lo:hi, :],
+                    in1=tb[q][:].rearrange("p u h d -> p (u h) d")[:, lo:hi, :],
                     op=ALU.add,
                 )
 
-        def nope_out(k, on_vector=False):
-            r, u = k // RUN, k % RUN
-            nh = groups[k // MT][1]
-            eng_copy = nc.vector.tensor_copy if on_vector else nc.scalar.copy
-            eng_copy(out=out_tile(r)[:, u, :, 0:NOPE], in_=acc_n[k].rearrange("p (h d) -> p h d", h=nh))
-
-        def nope_out_pair(k):
-            nh = groups[k // MT][1]
-            nc.scalar.copy(out=out_tile(k // RUN)[:, :, :, 0:NOPE], in_=acc_pair[k][:].rearrange("p u (h d) -> p u h d", h=nh))
+        def nope_out_pair(q):
+            nh = nh_pair(q)
+            nc.scalar.copy(out=out_tile(q)[:, :, :, 0:NOPE], in_=acc_pair[2 * q][:].rearrange("p u (h d) -> p u h d", h=nh))
 
         def store(k):
             j, m = k // MT, k % MT
             h0, nh = groups[j]
-            nc.sync.dma_start(out=out_v[m][:, h0 * QK : (h0 + nh) * QK], in_=ot[k // RUN][:, k % RUN, :, :].rearrange("p h d -> p (h d)"))
+            nc.sync.dma_start(out=out_v[m][:, h0 * QK : (h0 + nh) * QK], in_=ot[k // 2][:, k % 2, :, :].rearrange("p h d -> p (h d)"))
 
-        n_runs = n // RUN
+        n_runs = len(runs)
+        win_at = dict((WIN_STEP[i], i) for i in range(n_runs))
+        run_of = {}
+        for i in range(n_runs):
+            for k in runs[i]:
+                run_of[k] = i
 
-        def quant_chunk(c):
-            return c if c >= MERGE_R_UNTIL else c + 1 - c % 2
+        def open_rows(i):
+            q0 = runs[i][0] // 2
+            pairs = [q0] if len(runs[i]) == 2 else [q0, q0 + 1]
+            return pairs
 
-        def pass_from(k):
-            if RUN == 2:
-                return k + ROPE_LAG - 3
-            return ((k - MT) // RUN) * RUN + ROPE_LAG + 1 + max(0, k % MT - 1)
+        def close_run(i, last):
+            pairs = open_rows(i)
+            for q in pairs:
+                rows = 2 * nh_pair(q)
+                lo = 0
+                if q == pairs[0] and OWN_G[i] > 0:
+                    lo = OWN_G[i]
+                elif q == pairs[-1] and not last:
+                    lo = LEFT_G[i + 1]
+                if last and SPLIT_LAST:
+                    for u in range(2):
+                        rope_add(q, nc.vector, max(lo, u * rows // 2), (u + 1) * rows // 2)
+                else:
+                    rope_add(q, nc.vector, lo, rows)
 
-        last_step = n + ROPE_LAG + 2 * RUN + 2
+        add_step = {}
+        for i in range(n_runs):
+            nxt = WIN_STEP[i + 1] if i + 1 < n_runs else WIN_STEP[i]
+            for k in runs[i]:
+                add_step[k] = nxt
+
+        def quant_step(c):
+            lag = EVAC_LAG + 1 if c in PE_ROPE else 1
+            if c < MERGE_UNTIL:
+                odd = c + 1 - c % 2
+                return odd + max(EVAC_LAG + 1 if odd in PE_ROPE else 1, EVAC_LAG if c in PE_ROPE else 0)
+            return c + lag
+
+        def pass_step(k, g):
+            j = k // MT
+            c = j * G + g
+            base = quant_step(c) + 1
+            i = run_of[k]
+            if k >= MT:
+                base = max(base, WIN_STEP[run_of[k - MT]] + 1)
+            else:
+                base = max(base, k + 2 + HS_STEP)
+            return base
+
+        last_step = 40
         for s in range(last_step):
             if s < n:
-                for t in range(C_PLANES[s]):
-                    cast_plane(s, t)
-                for t in range(C_PLANES[s], PACK - V_PLANES[s]):
+                for t in range(PACK - V_PLANES[s]):
                     widen(s, t, False)
-                for t in range(C_PLANES[s]):
-                    scale_plane(s, t)
-                if s >= S_INTER_FROM:
-                    inter_s(s, S_INTER_HEADS)
-            for c in range(0 if s == 0 else s + VW_AHEAD, min(n, s + VW_AHEAD + 1)):
-                for t in range(PACK - V_PLANES[c], PACK):
-                    widen(c, t, True)
+                if s in S_INTER:
+                    inter_s(s, S_INTER[s])
+                for t in range(PACK - V_PLANES[s], PACK):
+                    widen(s, t, True)
             c = s - 1
             if PE_FROM <= c < n:
-                ident_nope(c)
+                ident_chunk(c)
             m = s - 1 - HS_STEP
             if 0 <= m < MT:
                 hs_copy(m, 0)
                 hs_copy(m, 1)
             c = s - 1
             if 0 <= c < n:
-                inter_rope_v(c, S_INTER_HEADS if c >= S_INTER_FROM else 0)
+                inter_rope_v(c, S_INTER.get(c, 1 if c in PE_ROPE else 0))
                 if c < PE_FROM:
                     inter_nope_v(c)
             c = s - EVAC_LAG
             if PE_FROM <= c < n:
-                evac_nope(c)
+                evac_chunk(c)
             if s == TABLE_STEP:
                 tables()
             c = s - 1 - EVAC_LAG
             if 0 <= c < n and c % G == G - 1:
                 quant_nope(c // G)
-            k0 = s - ROPE_LAG
-            if k0 >= 0 and k0 % RUN == 0 and k0 < n:
-                r = k0 // RUN
-                rows = RUN * groups[k0 // MT][1]
-                if r > 0:
-                    prows = RUN * groups[(k0 - RUN) // MT][1]
-                    grows = min(prows - 1, G_ROWS_BY_WINDOW[groups[k0 // MT][1]])
-                    if r >= n_runs - LAST_NO_G:
-                        grows = 0
-                    rope_add(r - 1, nc.vector, grows, prows)
-                    if grows > 0:
-                        nc.gpsimd.tensor_copy(out=gate[:], in_=ot[r - 1][:, RUN - 1, groups[(k0 - RUN) // MT][1] - 1, QK - 1 : QK])
-                        rope_add(r - 1, nc.gpsimd, 0, grows)
-                    if NOUT_ON_V:
-                        for u in range(RUN):
-                            nope_out(k0 - RUN + u, True)
-                for u in range(RUN):
-                    rope_mults(k0 + u)
-                if r == n_runs - 1:
-                    for u in range(RUN):
-                        rope_add(r, nc.vector, u * rows // RUN, (u + 1) * rows // RUN)
-            c = s - QR_LAG
-            if 0 <= c < n:
-                if c >= MERGE_R_UNTIL:
-                    quant_rope(c, False)
-                elif c % 2 == 1:
-                    quant_rope(c, True)
+            if s in win_at:
+                i = win_at[s]
+                if i > 0:
+                    q = open_rows(i - 1)[-1]
+                    if LEFT_G[i] > 0 and GATE == "early":
+                        nc.vector.memset(out_tile(q)[:, 0, 0, NOPE : NOPE + 1], 0.0)
+                    close_run(i - 1, False)
+                    if LEFT_G[i] > 0:
+                        if GATE == "memset":
+                            nc.vector.memset(ot[q][:, 0, 0, NOPE : NOPE + 1], 0.0)
+                        elif GATE == "copy":
+                            nc.gpsimd.tensor_copy(out=gate[:], in_=ot[q][:, 1, nh_pair(q) - 1, QK - 1 : QK])
+                        rope_add(q, nc.gpsimd, 0, LEFT_G[i])
+                for k in runs[i]:
+                    rope_mults(k)
+                if OWN_G[i] > 0:
+                    rope_add(open_rows(i)[0], nc.gpsimd, 0, OWN_G[i])
+                if i == n_runs - 1:
+                    close_run(i, True)
+            for c in range(n):
+                if quant_step(c) == s:
+                    if c >= MERGE_UNTIL:
+                        quant_rope(c, False)
+                    elif c % 2 == 1:
+                        quant_rope(c, True)
             m = s - 1 - HS_STEP
             if 0 <= m < MT:
                 hs_quant(m)
@@ -439,20 +473,18 @@ def tile_multilatentattention_pb_kernel(tc, hidden_states, rope_cos, rope_sin, W
                 hs_transposes(m)
             for k in range(n):
                 for g in range(G):
-                    if max(quant_chunk((k // MT) * G + g) + PASS_LAG, pass_from(k), (k + 2 + HS_STEP) if k < MT else 0) == s:
+                    if pass_step(k, g) == s:
                         mm_pass(k, True, g)
             for k in range(n):
                 j, m = k // MT, k % MT
-                if j * G + 5 + EVAC_LAG + m // 2 == s:
+                if NOPE_STEP[j] + m // 2 == s:
                     for g in range(G):
                         mm_pass(k, False, g)
+            for q in range(n // 2):
+                j, m = 2 * q // MT, 2 * q % MT
+                if NOPE_STEP[j] + m // 2 + NOUT_LAG == s:
+                    nope_out_pair(q)
             for k in range(n):
                 j, m = k // MT, k % MT
-                if j * G + 5 + EVAC_LAG + m // 2 + NOUT_LAG == s and k % 2 == 0:
-                    nope_out_pair(k)
-            for k in range(n):
-                r = k // RUN
-                j, m = k // MT, k % MT
-                add_step = (r + 1) * RUN + ROPE_LAG if r < n_runs - 1 else r * RUN + ROPE_LAG
-                if max(add_step, j * G + 5 + EVAC_LAG + m // 2 + NOUT_LAG) == s:
+                if max(add_step[k], NOPE_STEP[j] + m // 2 + NOUT_LAG) == s:
                     store(k)

@@ -26,8 +26,8 @@ FLOPS = 2 * T * HID * H * QK
 GROUP_HEADS = (4, 4, 4, 2, 2)
 N_CHUNKS = 20
 RUN_UNITS = (2,) * 10
-V_PLANES = (2, 2, 2, 2, 1, 1, 1, 0, 1, 0, 0, 0, 0, 0, 0, 0, 0, 0, 0, 0)
-PE_FROM = 4
+V_PLANES = (2,) * 7 + (0,) * 13
+PE_FROM = 0
 PE_ROPE = ()
 EVAC_LAG = 2
 HS_STEP = 2

@@ -182,22 +182,22 @@ def tile_multilatentattention_pb_kernel(tc, hidden_states, rope_cos, rope_sin, W
 
         def ident_chunk(c):
             nh = heads_of(c)
-            view = planes[c][:].rearrange("p t (h d) -> p h d t", d=QK)
+            view = planes[c][:].rearrange("p t (h d) -> p h t d", d=QK)
             rope_head = 1 if c in PE_ROPE else 0
             pis[c] = ps.tile([P, nh * NOPE * PACK + rope_head * ROPE * PACK], BF16, name="pi", tag="misc", bufs=2)
             for a in range(nh // 2):
                 nc.tensor.matmul(
-                    out=pis[c][:, a * 512 : (a + 1) * 512].rearrange("p (h d t) -> p h d t", h=2, t=PACK),
+                    out=pis[c][:, a * 512 : (a + 1) * 512].rearrange("p (h d t) -> p h t d", h=2, t=PACK),
                     lhsT=ident_b[:],
-                    rhs=view[:, 2 * a : 2 * a + 2, 0:NOPE, :],
+                    rhs=view[:, 2 * a : 2 * a + 2, :, 0:NOPE],
                     start=True,
                     stop=True,
                 )
             if rope_head:
                 nc.tensor.matmul(
-                    out=pis[c][:, nh * 256 : nh * 256 + 512].rearrange("p (d t) -> p d t", t=PACK),
+                    out=pis[c][:, nh * 256 : nh * 256 + 512].rearrange("p (d t) -> p t d", t=PACK),
                     lhsT=ident_b[:],
-                    rhs=view[:, nh - 1, NOPE:QK, :],
+                    rhs=view[:, nh - 1, :, NOPE:QK],
                     start=True,
                     stop=True,
                 )

@@ -26,7 +26,7 @@ FLOPS = 2 * T * HID * H * QK
 GROUP_HEADS = (4, 4, 4, 2, 2)
 N_CHUNKS = 20
 RUN_UNITS = (2,) * 10
-V_PLANES = (2,) * 7 + (0,) * 13
+V_PLANES = (2,) * 7 + (1,) + (0,) * 12
 PE_FROM = 0
 PE_ROPE = ()
 EVAC_LAG = 2
@@ -38,16 +38,21 @@ OT_BUFS = 4
 TAB_BUFS = 3
 WC_BUFS = 2
 GRPR_BUFS = 2
-S_INTER = {18: 1, 19: 1}
+S_INTER = {19: 1}
 WIN_STEP = tuple(range(6, 26, 2))
 PASS_STEP = {}
 NOPE_STEP = (7, 11, 15, 19, 23)
 NOUT_LAG = 3
-LEFT_G = (0, 6, 6, 6, 6, 6, 2, 2, 2, 0)
+LEFT_G = (0, 7, 7, 7, 7, 7, 3, 3, 3, 0)
 OWN_G = (0,) * 10
 GATE = "early"
 MERGE_UNTIL = 20
 SPLIT_LAST = True
+NOPE_FIRST = True
+BY_PLANE = (0,)
+PLANE_ORDER = (0, 1, 2, 3)
+SC_ON = "sync"
+V_NOPE = ()
 
 
 def tile_multilatentattention_pb_kernel(tc, hidden_states, rope_cos, rope_sin, Wq_bytes, Wq_scale, out):
@@ -122,9 +127,9 @@ def tile_multilatentattention_pb_kernel(tc, hidden_states, rope_cos, rope_sin, W
             j, g = c // G, c % G
             h0, nh = groups[j]
             cols = slice(h0 * QK, (h0 + nh) * QK)
-            if c == 0:
+            if c in BY_PLANE:
                 wb[c] = [None] * PACK
-                for t in range(PACK):
+                for t in PLANE_ORDER:
                     one = const.tile([P, nh * QK], U8, name="wq_bytes_%d_%d" % (c, t))
                     nc.sync.dma_start(out=one[:], in_=w_v[g][:, t, cols])
                     wb[c][t] = one[:]
@@ -137,7 +142,7 @@ def tile_multilatentattention_pb_kernel(tc, hidden_states, rope_cos, rope_sin, W
             hs_raw[m] = const.tile([P, HID], BF16, name="hs_raw_%d" % m)
             nc.sync.dma_start(out=hs_raw[m][:], in_=hs_v[m])
 
-        nc.sync.dma_start(out=sc[:], in_=sc_v)
+        (nc.gpsimd if SC_ON == "gpsimd" else nc.scalar if SC_ON == "scalar" else nc.sync).dma_start(out=sc[:], in_=sc_v)
         loaded = 0
         for item in LOAD_ORDER:
             if item == "cs":
@@ -411,6 +416,18 @@ def tile_multilatentattention_pb_kernel(tc, hidden_states, rope_cos, rope_sin, W
                 base = max(base, k + 2 + HS_STEP)
             return base
 
+        def nope_passes(s):
+            for k in range(n):
+                j, m = k // MT, k % MT
+                if NOPE_STEP[j] + m // 2 == s:
+                    for g in range(G):
+                        mm_pass(k, False, g)
+
+        for k in range(n):
+            for g in range(G):
+                assert pass_step(k, g) < WIN_STEP[run_of[k]], (k, g)
+            assert NOPE_STEP[k // MT] + (k % MT) // 2 + NOUT_LAG > 0
+
         last_step = 40
         for s in range(last_step):
             if s < n:
@@ -421,7 +438,7 @@ def tile_multilatentattention_pb_kernel(tc, hidden_states, rope_cos, rope_sin, W
                 for t in range(PACK - V_PLANES[s], PACK):
                     widen(s, t, True)
             c = s - 1
-            if PE_FROM <= c < n:
+            if PE_FROM <= c < n and c not in V_NOPE:
                 ident_chunk(c)
             m = s - 1 - HS_STEP
             if 0 <= m < MT:
@@ -430,10 +447,10 @@ def tile_multilatentattention_pb_kernel(tc, hidden_states, rope_cos, rope_sin, W
             c = s - 1
             if 0 <= c < n:
                 inter_rope_v(c, S_INTER.get(c, 1 if c in PE_ROPE else 0))
-                if c < PE_FROM:
+                if c < PE_FROM or c in V_NOPE:
                     inter_nope_v(c)
             c = s - EVAC_LAG
-            if PE_FROM <= c < n:
+            if PE_FROM <= c < n and c not in V_NOPE:
                 evac_chunk(c)
             if s == TABLE_STEP:
                 tables()
@@ -471,15 +488,14 @@ def tile_multilatentattention_pb_kernel(tc, hidden_states, rope_cos, rope_sin, W
             m = s - HS_STEP
             if 0 <= m < MT:
                 hs_transposes(m)
+            if NOPE_FIRST:
+                nope_passes(s)
             for k in range(n):
                 for g in range(G):
                     if pass_step(k, g) == s:
                         mm_pass(k, True, g)
-            for k in range(n):
-                j, m = k // MT, k % MT
-                if NOPE_STEP[j] + m // 2 == s:
-                    for g in range(G):
-                        mm_pass(k, False, g)
+            if not NOPE_FIRST:
+                nope_passes(s)
             for q in range(n // 2):
                 j, m = 2 * q // MT, 2 * q % MT
                 if NOPE_STEP[j] + m // 2 + NOUT_LAG == s:

@@ -33,13 +33,13 @@ EVAC_LAG = 2
 HS_STEP = 2
 LOAD_ORDER = ("w0", "w1", "w2", "h0", "w3", "h1", "cs", "w4", "h2", "w5", "h3")
 TABLE_STEP = 4
-PLANE_BUFS = 5
+PLANE_BUFS = 6
 OT_BUFS = 4
 TAB_BUFS = 3
 WC_BUFS = 2
 GRPR_BUFS = 2
 S_INTER = {19: 1}
-WIN_STEP = tuple(range(6, 26, 2))
+WIN_STEP = (7, 8, 10, 12, 14, 16, 18, 20, 22, 24)
 PASS_STEP = {}
 NOPE_STEP = (7, 11, 15, 19, 23)
 NOUT_LAG = 3
@@ -49,8 +49,8 @@ GATE = "early"
 MERGE_UNTIL = 20
 SPLIT_LAST = True
 NOPE_FIRST = True
-BY_PLANE = (0,)
-PLANE_ORDER = (0, 1, 2, 3)
+BY_PLANE = (0, 1)
+PLANE_ORDER = (0, 2, 1, 3)
 SC_ON = "sync"
 V_NOPE = ()
 

@@ -49,6 +49,7 @@ GATE = "early"
 MERGE_UNTIL = 20
 SPLIT_LAST = True
 NOPE_FIRST = True
+RUN_COLS = 8
 BY_PLANE = (0, 1)
 PLANE_ORDER = (0, 2, 1, 3)
 SC_ON = "sync"
@@ -181,8 +182,8 @@ def tile_multilatentattention_pb_kernel(tc, hidden_states, rope_cos, rope_sin, W
             if skip == nh:
                 return
             nc.vector.tensor_copy(
-                out=rope_part(c).rearrange("p (h c i t) -> p h c t i", h=nh, i=4, t=PACK)[:, 0 : nh - skip],
-                in_=planes[c][:].rearrange("p t (h d) -> p t h d", d=QK)[:, :, 0 : nh - skip, NOPE:QK].rearrange("p t h (c i) -> p h c t i", i=4),
+                out=rope_part(c).rearrange("p (h c i t) -> p h c t i", h=nh, i=RUN_COLS, t=PACK)[:, 0 : nh - skip],
+                in_=planes[c][:].rearrange("p t (h d) -> p t h d", d=QK)[:, :, 0 : nh - skip, NOPE:QK].rearrange("p t h (c i) -> p h c t i", i=RUN_COLS),
             )
 
         def ident_chunk(c):

from contextlib import ExitStack

import concourse.mybir as mybir
from concourse.masks import make_identity

F32 = mybir.dt.float32
BF16 = mybir.dt.bfloat16
U32 = mybir.dt.uint32
U8 = mybir.dt.uint8
FP8 = mybir.dt.float8_e4m3fn
FP8X4 = mybir.dt.float8_e4m3fn_x4
ALU = mybir.AluOpType
ACT = mybir.ActivationFunctionType

T, HID, H, NOPE, ROPE = 512, 2048, 16, 64, 128
QK = NOPE + ROPE
HALF = ROPE // 2
P = 128
PACK = 4
K_PASS = P * PACK
G = HID // K_PASS
MT = T // P

FLOPS = 2 * T * HID * H * QK

GROUP_HEADS = (4, 4, 4, 2, 2)
N_CHUNKS = 20
RUN_UNITS = (2,) * 10
V_PLANES = (2,) * 7 + (1,) + (0,) * 12
PE_FROM = 0
PE_ROPE = ()
EVAC_LAG = 2
HS_STEP = 2
LOAD_ORDER = ("w0", "w1", "w2", "h0", "w3", "h1", "cs", "w4", "h2", "w5", "h3")
TABLE_STEP = 4
PLANE_BUFS = 6
OT_BUFS = 4
TAB_BUFS = 3
WC_BUFS = 2
GRPR_BUFS = 2
S_INTER = {19: 1}
WIN_STEP = (7, 8, 10, 12, 14, 16, 18, 20, 22, 24)
PASS_STEP = {}
NOPE_STEP = (7, 11, 15, 19, 23)
NOUT_LAG = 3
LEFT_G = (0, 7, 7, 7, 7, 7, 3, 3, 3, 0)
OWN_G = (0,) * 10
GATE = "early"
MERGE_UNTIL = 20
SPLIT_LAST = True
NOPE_FIRST = True
RUN_COLS = 8
BY_PLANE = (0, 1)
PLANE_ORDER = (0, 2, 1, 3)
SC_ON = "sync"
V_NOPE = ()


def tile_multilatentattention_pb_kernel(tc, hidden_states, rope_cos, rope_sin, Wq_bytes, Wq_scale, out):
    nc = tc.nc
    hs_v = hidden_states.rearrange("b (m p) k -> (b m) p k", p=P)
    w_v = Wq_bytes.rearrange("(g p t) n -> g p t n", p=P, t=PACK)
    sc_v = Wq_scale.rearrange("(g p t) o -> p g (t o)", p=P, t=PACK)
    cos_v = rope_cos.rearrange("(m p) i -> p m i", p=P)
    sin_v = rope_sin.rearrange("(m p) i -> p m i", p=P)
    out_v = out.rearrange("b (m p) h d -> (b m) p (h d)", p=P)

    groups = []
    first = 0
    for heads in GROUP_HEADS:
        groups.append((first, heads))
        first += heads
    n = N_CHUNKS
    runs = []
    first = 0
    for units in RUN_UNITS:
        runs.append(list(range(first, first + units)))
        first += units

    with ExitStack() as ctx:
        const = ctx.enter_context(tc.tile_pool(name="const", bufs=1))
        work = ctx.enter_context(tc.tile_pool(name="work", bufs=3))
        ps = ctx.enter_context(tc.psum_pool(name="ps", bufs=2))

        ident_f = const.tile([P, P], F32, name="ident_f")
        make_identity(nc, ident_f[:])
        ident_b = const.tile([P, P], BF16, name="ident_b")
        make_identity(nc, ident_b[:])

        ctx.enter_context(tc.manual_schedule())

        warm_i = const.tile([P, 1], F32, name="warm_i")
        warm_o = const.tile([P, 1], F32, name="warm_o")
        gate = const.tile([P, 1], F32, name="gate")
        sign = const.tile([P, 2], F32, name="sign")
        nc.vector.memset(warm_i[:], 0.0)
        nc.vector.memset(sign[:, 0:1], -1.0)
        nc.vector.memset(sign[:, 1:2], 1.0)
        nc.scalar.activation(out=warm_o[:], in_=warm_i[:], func=ACT.Copy)

        sc = const.tile([P, G, PACK], F32, name="sc")
        cos_sb = const.tile([P, MT, HALF], BF16, name="cos_sb")
        sin_sb = const.tile([P, MT, HALF], BF16, name="sin_sb")
        s2 = const.tile([P, MT, ROPE], F32, name="s2")
        hs_codes = const.tile([P, MT, G * P], U32, name="hs_codes", align_bytes=64)
        hs_scales = const.tile([P, MT, G * P], U8, name="hs_scales", align_bytes=64)

        wb = {}
        hs_raw = {}
        planes = {}
        grp_r = {}
        grp_n = {}
        pis = {}
        wc = {}
        xts = {}
        hs_grp = {}
        acc_r = {}
        acc_n = {}
        acc_pair = {}
        ta = {}
        tb = {}
        ot = {}

        def heads_of(c):
            return groups[c // G][1]

        def load_w(c):
            j, g = c // G, c % G
            h0, nh = groups[j]
            cols = slice(h0 * QK, (h0 + nh) * QK)
            if c in BY_PLANE:
                wb[c] = [None] * PACK
                for t in PLANE_ORDER:
                    one = const.tile([P, nh * QK], U8, name="wq_bytes_%d_%d" % (c, t))
                    nc.sync.dma_start(out=one[:], in_=w_v[g][:, t, cols])
                    wb[c][t] = one[:]
            else:
                whole = const.tile([P, PACK, nh * QK], U8, name="wq_bytes_%d" % c)
                nc.sync.dma_start(out=whole[:], in_=w_v[g][:, :, cols])
                wb[c] = [whole[:, t, :] for t in range(PACK)]

        def load_hs(m):
            hs_raw[m] = const.tile([P, HID], BF16, name="hs_raw_%d" % m)
            nc.sync.dma_start(out=hs_raw[m][:], in_=hs_v[m])

        (nc.gpsimd if SC_ON == "gpsimd" else nc.scalar if SC_ON == "scalar" else nc.sync).dma_start(out=sc[:], in_=sc_v)
        loaded = 0
        for item in LOAD_ORDER:
            if item == "cs":
                nc.sync.dma_start(out=cos_sb[:], in_=cos_v)
                nc.sync.dma_start(out=sin_sb[:], in_=sin_v)
            elif item.startswith("w"):
                load_w(int(item[1:]))
                loaded += 1
            else:
                load_hs(int(item[1:]))
        for c in range(loaded, n):
            load_w(c)

        def widen(c, t, on_vector):
            g = c % G
            nh = heads_of(c)
            if c not in planes:
                planes[c] = work.tile([P, PACK, nh * QK], BF16, name="planes", tag="planes", bufs=PLANE_BUFS)
            src = wb[c][t].bitcast(FP8)
            dst = planes[c][:, t, :]
            if on_vector:
                nc.vector.tensor_scalar(out=dst, in0=src, scalar1=sc[:, g, t : t + 1], scalar2=None, op0=ALU.mult)
            else:
                nc.scalar.activation(out=dst, in_=src, func=ACT.Copy, scale=sc[:, g, t : t + 1])

        def inter_s(c, heads):
            nh = heads_of(c)
            for h in range(nh - heads, nh):
                nc.scalar.copy(
                    out=rope_part(c).rearrange("p (h c i t) -> p h c t i", h=nh, i=4, t=PACK)[:, h],
                    in_=planes[c][:].rearrange("p t (h d) -> p t h d", d=QK)[:, :, h, NOPE:QK].rearrange("p t (c i) -> p c t i", i=4),
                )

        def inter_rope_v(c, skip):
            nh = heads_of(c)
            if skip == nh:
                return
            nc.vector.tensor_copy(
                out=rope_part(c).rearrange("p (h c i t) -> p h c t i", h=nh, i=RUN_COLS, t=PACK)[:, 0 : nh - skip],
                in_=planes[c][:].rearrange("p t (h d) -> p t h d", d=QK)[:, :, 0 : nh - skip, NOPE:QK].rearrange("p t h (c i) -> p h c t i", i=RUN_COLS),
            )

        def ident_chunk(c):
            nh = heads_of(c)
            view = planes[c][:].rearrange("p t (h d) -> p h t d", d=QK)
            rope_head = 1 if c in PE_ROPE else 0
            pis[c] = ps.tile([P, nh * NOPE * PACK + rope_head * ROPE * PACK], BF16, name="pi", tag="misc", bufs=2)
            for a in range(nh // 2):
                nc.tensor.matmul(
                    out=pis[c][:, a * 512 : (a + 1) * 512].rearrange("p (h d t) -> p h t d", h=2, t=PACK),
                    lhsT=ident_b[:],
                    rhs=view[:, 2 * a : 2 * a + 2, :, 0:NOPE],
                    start=True,
                    stop=True,
                )
            if rope_head:
                nc.tensor.matmul(
                    out=pis[c][:, nh * 256 : nh * 256 + 512].rearrange("p (d t) -> p t d", t=PACK),
                    lhsT=ident_b[:],
                    rhs=view[:, nh - 1, :, NOPE:QK],
                    start=True,
                    stop=True,
                )

        def nope_part(c):
            j = c // G
            if j not in grp_n:
                grp_n[j] = work.tile([P, G, groups[j][1] * NOPE * PACK], BF16, name="grp_n", tag="grp_n", bufs=2, align_bytes=64)
            return grp_n[j][:, c % G, :]

        def evac_chunk(c):
            nh = heads_of(c)
            if c in PE_ROPE:
                nc.scalar.copy(out=rope_part(c)[:, (nh - 1) * 512 : nh * 512], in_=pis[c][:, nh * 256 : nh * 256 + 512])
            nc.scalar.copy(out=nope_part(c), in_=pis[c][:, 0 : nh * 256])

        def inter_nope_v(c):
            nh = heads_of(c)
            nc.vector.tensor_copy(
                out=nope_part(c).rearrange("p (h c i t) -> p h c t i", h=nh, i=4, t=PACK),
                in_=planes[c][:].rearrange("p t (h d) -> p t h d", d=QK)[:, :, :, 0:NOPE].rearrange("p t h (c i) -> p h c t i", i=4),
            )

        def rope_part(c):
            q = c // 2
            if q not in grp_r:
                grp_r[q] = work.tile([P, 2, heads_of(c) * ROPE * PACK], BF16, name="grp_r", tag="grp_r", bufs=GRPR_BUFS, align_bytes=64)
            return grp_r[q][:, c % 2, :]

        def codes_of(j):
            if j not in wc:
                nh = groups[j][1]
                wc[j] = (
                    work.tile([P, G, nh * ROPE], U32, name="wc_r", tag="wc_r", bufs=WC_BUFS, align_bytes=64),
                    work.tile([P, G, nh * ROPE], U8, name="ws_r", tag="ws_r", bufs=WC_BUFS, align_bytes=64),
                    work.tile([P, G, nh * NOPE], U32, name="wc_n", tag="wc_n", bufs=WC_BUFS, align_bytes=64),
                    work.tile([P, G, nh * NOPE], U8, name="ws_n", tag="ws_n", bufs=WC_BUFS, align_bytes=64),
                )
            return wc[j]

        def quant_rope(c, both):
            j, g = c // G, c % G
            t = codes_of(j)
            if both:
                nc.vector.quantize_mx(
                    out=t[0][:, g - 1 : g + 1, :].rearrange("p g x -> p (g x)").bitcast(FP8X4),
                    scales=t[1][:, g - 1 : g + 1, :].rearrange("p g x -> p (g x)"),
                    in_=grp_r[c // 2][:].rearrange("p g x -> p (g x)"),
                )
            else:
                nc.vector.quantize_mx(out=t[0][:, g, :].bitcast(FP8X4), scales=t[1][:, g, :], in_=rope_part(c))

        def quant_nope(j):
            t = codes_of(j)
            nc.vector.quantize_mx(
                out=t[2][:].rearrange("p g x -> p (g x)").bitcast(FP8X4),
                scales=t[3][:].rearrange("p g x -> p (g x)"),
                in_=grp_n[j][:].rearrange("p g x -> p (g x)"),
            )

        def hs_transposes(m):
            words = hs_raw[m][:].bitcast(F32)
            xts[m] = []
            for half in range(2):
                xt = ps.tile([P, 2, 2, P], F32, name="xt", tag=("misc", "acc_n")[half], bufs=2)
                for g2 in range(2):
                    g = 2 * half + g2
                    for u in range(2):
                        nc.tensor.transpose(xt[:, g2, u, :], words[:, 256 * g + u : 256 * (g + 1) : 2], ident_f[:])
                xts[m].append(xt)

        def hs_copy(m, half):
            if m not in hs_grp:
                hs_grp[m] = work.tile([P, G * P * PACK], BF16, name="hs_grp", tag="hs_grp", bufs=2, align_bytes=64)
            dst = hs_grp[m][:].bitcast(F32).rearrange("p (g r u) -> p g r u", g=G, u=2)
            nc.scalar.copy(out=dst[:, 2 * half : 2 * half + 2, :, :], in_=xts[m][half][:].rearrange("p g u r -> p g r u"))

        def hs_quant(m):
            nc.vector.quantize_mx(out=hs_codes[:, m, :].bitcast(FP8X4), scales=hs_scales[:, m, :], in_=hs_grp[m][:])

        def tables():
            nc.vector.tensor_tensor(
                out=s2[:].rearrange("p m (i e) -> p (m i) e", e=2),
                in0=sin_sb[:].rearrange("p m i -> p (m i)").unsqueeze(2).to_broadcast([P, MT * HALF, 2]),
                in1=sign[:].unsqueeze(1).to_broadcast([P, MT * HALF, 2]),
                op=ALU.mult,
            )

        def mm_pass(k, rope, g):
            j, m = k // MT, k % MT
            nh = groups[j][1]
            t = codes_of(j)
            if rope:
                if k not in acc_r:
                    acc_r[k] = ps.tile([P, nh * ROPE], F32, name="acc_r", tag="acc_r", bufs=4)
                acc, cod, sca = acc_r[k][:], t[0], t[1]
            else:
                if k % 2 == 0 and k not in acc_n:
                    pair = ps.tile([P, 2, nh * NOPE], F32, name="acc_n", tag="acc_n", bufs=2)
                    acc_n[k] = pair[:, 0, :]
                    acc_n[k + 1] = pair[:, 1, :]
                    acc_pair[k] = pair
                acc, cod, sca = acc_n[k], t[2], t[3]
            nc.tensor.matmul_mx(
                out=acc,
                lhsT=hs_codes[:, m, g * P : (g + 1) * P].bitcast(FP8X4),
                lhsT_scale=hs_scales[:, m, g * P : (g + 1) * P],
                rhs=cod[:, g, :].bitcast(FP8X4),
                rhs_scale=sca[:, g, :],
                start=(g == 0),
                stop=(g == G - 1),
            )

        def nh_pair(q):
            return groups[2 * q // MT][1]

        def pair_tiles(q):
            nh = nh_pair(q)
            if q not in ta:
                ta[q] = work.tile([P, 2, nh, ROPE], F32, name="ta", tag="ta", bufs=TAB_BUFS)
                tb[q] = work.tile([P, 2, nh, ROPE], F32, name="tb", tag="tb", bufs=TAB_BUFS)
            return nh

        def out_tile(q):
            if q not in ot:
                ot[q] = work.tile([P, 2, nh_pair(q), QK], F32, name="ot", tag="ot", bufs=OT_BUFS)
            return ot[q]

        def rope_mults(k):
            q, u, m = k // 2, k % 2, k % MT
            nh = pair_tiles(q)
            nc.vector.tensor_tensor(
                out=ta[q][:, u, :, :].rearrange("p h (i e) -> p h i e", e=2),
                in0=acc_r[k][:].rearrange("p (h i e) -> p h i e", h=nh, e=2),
                in1=cos_sb[:, m, :].unsqueeze(1).unsqueeze(3).to_broadcast([P, nh, HALF, 2]),
                op=ALU.mult,
            )
            nc.vector.tensor_tensor(
                out=tb[q][:, u, :, :].rearrange("p h (i e) -> p h i e", e=2),
                in0=acc_r[k][:].rearrange("p (h i e) -> p h i e", h=nh, e=2)[:, :, :, ::-1],
                in1=s2[:, m, :].rearrange("p (i e) -> p i e", e=2).unsqueeze(1).to_broadcast([P, nh, HALF, 2]),
                op=ALU.mult,
            )

        def rope_add(q, eng, lo, hi):
            if hi > lo:
                eng.tensor_tensor(
                    out=out_tile(q)[:].rearrange("p u h d -> p (u h) d")[:, lo:hi, NOPE:QK],
                    in0=ta[q][:].rearrange("p u h d -> p (u h) d")[:, lo:hi, :],
                    in1=tb[q][:].rearrange("p u h d -> p (u h) d")[:, lo:hi, :],
                    op=ALU.add,
                )

        def nope_out_pair(q):
            nh = nh_pair(q)
            nc.scalar.copy(out=out_tile(q)[:, :, :, 0:NOPE], in_=acc_pair[2 * q][:].rearrange("p u (h d) -> p u h d", h=nh))

        def store(k):
            j, m = k // MT, k % MT
            h0, nh = groups[j]
            nc.sync.dma_start(out=out_v[m][:, h0 * QK : (h0 + nh) * QK], in_=ot[k // 2][:, k % 2, :, :].rearrange("p h d -> p (h d)"))

        n_runs = len(runs)
        win_at = dict((WIN_STEP[i], i) for i in range(n_runs))
        run_of = {}
        for i in range(n_runs):
            for k in runs[i]:
                run_of[k] = i

        def open_rows(i):
            q0 = runs[i][0] // 2
            pairs = [q0] if len(runs[i]) == 2 else [q0, q0 + 1]
            return pairs

        def close_run(i, last):
            pairs = open_rows(i)
            for q in pairs:
                rows = 2 * nh_pair(q)
                lo = 0
                if q == pairs[0] and OWN_G[i] > 0:
                    lo = OWN_G[i]
                elif q == pairs[-1] and not last:
                    lo = LEFT_G[i + 1]
                if last and SPLIT_LAST:
                    for u in range(2):
                        rope_add(q, nc.vector, max(lo, u * rows // 2), (u + 1) * rows // 2)
                else:
                    rope_add(q, nc.vector, lo, rows)

        add_step = {}
        for i in range(n_runs):
            nxt = WIN_STEP[i + 1] if i + 1 < n_runs else WIN_STEP[i]
            for k in runs[i]:
                add_step[k] = nxt

        def quant_step(c):
            lag = EVAC_LAG + 1 if c in PE_ROPE else 1
            if c < MERGE_UNTIL:
                odd = c + 1 - c % 2
                return odd + max(EVAC_LAG + 1 if odd in PE_ROPE else 1, EVAC_LAG if c in PE_ROPE else 0)
            return c + lag

        def pass_step(k, g):
            j = k // MT
            c = j * G + g
            base = quant_step(c) + 1
            i = run_of[k]
            if k >= MT:
                base = max(base, WIN_STEP[run_of[k - MT]] + 1)
            else:
                base = max(base, k + 2 + HS_STEP)
            return base

        def nope_passes(s):
            for k in range(n):
                j, m = k // MT, k % MT
                if NOPE_STEP[j] + m // 2 == s:
                    for g in range(G):
                        mm_pass(k, False, g)

        for k in range(n):
            for g in range(G):
                assert pass_step(k, g) < WIN_STEP[run_of[k]], (k, g)
            assert NOPE_STEP[k // MT] + (k % MT) // 2 + NOUT_LAG > 0

        last_step = 40
        for s in range(last_step):
            if s < n:
                for t in range(PACK - V_PLANES[s]):
                    widen(s, t, False)
                if s in S_INTER:
                    inter_s(s, S_INTER[s])
                for t in range(PACK - V_PLANES[s], PACK):
                    widen(s, t, True)
            c = s - 1
            if PE_FROM <= c < n and c not in V_NOPE:
                ident_chunk(c)
            m = s - 1 - HS_STEP
            if 0 <= m < MT:
                hs_copy(m, 0)
                hs_copy(m, 1)
            c = s - 1
            if 0 <= c < n:
                inter_rope_v(c, S_INTER.get(c, 1 if c in PE_ROPE else 0))
                if c < PE_FROM or c in V_NOPE:
                    inter_nope_v(c)
            c = s - EVAC_LAG
            if PE_FROM <= c < n and c not in V_NOPE:
                evac_chunk(c)
            if s == TABLE_STEP:
                tables()
            c = s - 1 - EVAC_LAG
            if 0 <= c < n and c % G == G - 1:
                quant_nope(c // G)
            if s in win_at:
                i = win_at[s]
                if i > 0:
                    q = open_rows(i - 1)[-1]
                    if LEFT_G[i] > 0 and GATE == "early":
                        nc.vector.memset(out_tile(q)[:, 0, 0, NOPE : NOPE + 1], 0.0)
                    close_run(i - 1, False)
                    if LEFT_G[i] > 0:
                        if GATE == "memset":
                            nc.vector.memset(ot[q][:, 0, 0, NOPE : NOPE + 1], 0.0)
                        elif GATE == "copy":
                            nc.gpsimd.tensor_copy(out=gate[:], in_=ot[q][:, 1, nh_pair(q) - 1, QK - 1 : QK])
                        rope_add(q, nc.gpsimd, 0, LEFT_G[i])
                for k in runs[i]:
                    rope_mults(k)
                if OWN_G[i] > 0:
                    rope_add(open_rows(i)[0], nc.gpsimd, 0, OWN_G[i])
                if i == n_runs - 1:
                    close_run(i, True)
            for c in range(n):
                if quant_step(c) == s:
                    if c >= MERGE_UNTIL:
                        quant_rope(c, False)
                    elif c % 2 == 1:
                        quant_rope(c, True)
            m = s - 1 - HS_STEP
            if 0 <= m < MT:
                hs_quant(m)
            m = s - HS_STEP
            if 0 <= m < MT:
                hs_transposes(m)
            if NOPE_FIRST:
                nope_passes(s)
            for k in range(n):
                for g in range(G):
                    if pass_step(k, g) == s:
                        mm_pass(k, True, g)
            if not NOPE_FIRST:
                nope_passes(s)
            for q in range(n // 2):
                j, m = 2 * q // MT, 2 * q % MT
                if NOPE_STEP[j] + m // 2 + NOUT_LAG == s:
                    nope_out_pair(q)
            for k in range(n):
                j, m = k // MT, k % MT
                if max(add_step[k], NOPE_STEP[j] + m // 2 + NOUT_LAG) == s:
                    store(k)
